import numpy as np
import ml_dtypes


def mxq(x, axis, fmt="e4m3"):
    dtype, down = {"e4m3": (ml_dtypes.float8_e4m3fn, 7), "e5m2": (ml_dtypes.float8_e5m2, 14)}[fmt]
    v = np.moveaxis(np.asarray(x, np.float32).astype(ml_dtypes.bfloat16).astype(np.float64), axis, -1)
    blocks = v.reshape(v.shape[:-1] + (-1, 32))
    amax = np.abs(blocks).max(-1, keepdims=True)
    byte = np.maximum(np.where(amax > 0, np.frexp(amax)[1] - 1 + 127, 0) - down, 1)
    scale = np.exp2(byte - 127.0)
    codes = (blocks / scale).astype(np.float32).astype(dtype).astype(np.float64)
    return np.moveaxis((codes * scale).reshape(v.shape), -1, axis)


WIDE = False


def mx_kscale(k):
    if not WIDE:
        return np.ones(k)
    levels = np.array([10, -10, 5, -5, 0])
    a = np.random.permutation(np.resize(levels, k // 512 * 4)).reshape(k // 512, 4)
    idx = np.arange(k)
    return np.exp2(a[idx // 512, idx % 128 // 32])


BF16 = ml_dtypes.bfloat16


def bf(x):
    return np.asarray(x, np.float32).astype(BF16)


def f64(x):
    return np.asarray(x).astype(np.float64)


E2M1 = np.array([0.0, 0.5, 1.0, 1.5, 2.0, 3.0, 4.0, 6.0, -0.0, -0.5, -1.0, -1.5, -2.0, -3.0, -4.0, -6.0])


def pack_weight(w, fmt):
    k, n = w.shape
    w = f64(bf(w)).reshape(k // 32, 32, n)
    amax = np.abs(w).max(1)
    if fmt == "e4m3":
        byte = np.frexp(amax)[1] - 1 + 127 - 7
    else:
        mant, ex = np.frexp(amax / 6.0)
        byte = np.where(mant > 0.5, ex, ex - 1) + 127
    byte = np.clip(np.where(amax > 0, byte, 1), 1, 254)
    scaled = (w * np.exp2(127.0 - byte)[:, None, :]).reshape(k, n).astype(np.float32)
    by_word = np.ascontiguousarray(scaled.reshape(k // 512, 128, 4, n).transpose(0, 1, 3, 2))
    if fmt == "e4m3":
        words = by_word.astype(ml_dtypes.float8_e4m3fn).view(np.uint8)
    else:
        c = by_word.astype(ml_dtypes.float4_e2m1fn).view(np.uint8) & 0xF
        words = c[..., 0::2] | (c[..., 1::2] << 4)
    return np.ascontiguousarray(words), np.ascontiguousarray(byte.astype(np.uint8).reshape(k // 512, 16, n))


def unpack_weight(words, scales, fmt):
    g, p, n, _ = words.shape
    if fmt == "e4m3":
        vals = np.ascontiguousarray(words).view(ml_dtypes.float8_e4m3fn).astype(np.float64)
    else:
        nib = np.empty((g, p, n, 4), np.uint8)
        nib[..., 0::2] = words & 0xF
        nib[..., 1::2] = words >> 4
        vals = E2M1[nib]
    vals = vals * np.repeat(np.exp2(scales.astype(np.float64) - 127.0), 8, axis=1)[..., None]
    return vals.transpose(0, 1, 3, 2).reshape(g * 512, n)


B, L, H, U = 2, 1024, 1024, 1024
R_MIN, R_MAX = 0.9, 0.999
FMT = "e4m3"


def setup_inputs():
    s, t = mx_kscale(H), mx_kscale(U)
    inputs = np.random.standard_normal((B, L, H)) * s
    Wi = np.random.standard_normal((U, H)) / np.sqrt(H) / s[None, :] * t[:, None]
    bi = np.random.standard_normal(U) * 0.03 * t
    Wo = np.random.standard_normal((H, U)) / np.sqrt(U) / t[None, :]
    bo = np.random.standard_normal(H) * 0.1
    r = np.random.uniform(size=U)
    nu_log = np.log(-0.5 * np.log(r * (R_MAX ** 2 - R_MIN ** 2) + R_MIN ** 2))
    gamma_log = np.log(np.sqrt(1.0 - np.exp(-np.exp(nu_log)) ** 2))
    params_log = np.stack([nu_log, gamma_log])
    Wi_words, Wi_scales = pack_weight(Wi.T, FMT)
    Wo_words, Wo_scales = pack_weight(Wo.T, FMT)
    return {"inputs": bf(inputs), "Wi_words": Wi_words, "Wi_scales": Wi_scales, "bi": bf(bi), "Wo_words": Wo_words, "Wo_scales": Wo_scales, "bo": bf(bo), "params_log": bf(params_log)}


def reference(inputs, Wi_words, Wi_scales, bi, Wo_words, Wo_scales, bo, params_log):
    u = (mxq(f64(inputs), 2, "e4m3") @ unpack_weight(Wi_words, Wi_scales, FMT)) + f64(bi)
    params = np.exp(f64(params_log))
    nu, gamma = params[0], params[1]

    log2_L = int(np.ceil(np.log2(L)))
    pad_len = 2 ** log2_L - L
    x = np.pad(u, ((0, 0), (0, pad_len), (0, 0))) if pad_len else u
    Lp = 2 ** log2_L

    for i in range(1, log2_L + 1):
        l = 2 ** i
        x = x.reshape(B * Lp // l, l, U)
        x1, x2 = x[:, : l // 2], x[:, l // 2:]
        pos = np.arange(1, l // 2 + 1, dtype=np.float64)
        lambs = np.exp(-pos[:, None] * nu)
        x2 = x2 + lambs * x1[:, -1:]
        x = np.concatenate([x1, x2], axis=1).reshape(B, Lp, U)

    x = x[:, :L] * gamma
    return (mxq(x, 2, "e4m3") @ unpack_weight(Wo_words, Wo_scales, FMT)) + f64(bo)

@@ -1,0 +1,272 @@
+from contextlib import ExitStack
+
+import concourse.mybir as mybir
+from concourse.masks import make_identity
+
+F32 = mybir.dt.float32
+BF16 = mybir.dt.bfloat16
+I32 = mybir.dt.int32
+U32 = mybir.dt.uint32
+U8 = mybir.dt.uint8
+FP8X4 = mybir.dt.float8_e4m3fn_x4
+ACT = mybir.ActivationFunctionType
+ALU = mybir.AluOpType
+
+BATCH, SEQ, FEAT, CHAN = 2, 1024, 1024, 1024
+
+P = 128
+PACK = 4
+K_PASS = P * PACK
+PASSES = FEAT // K_PASS
+WIDE = 512
+TOK_TILES = SEQ // P
+CHAN_TILES = CHAN // P
+TILES_PER_PASS = K_PASS // P
+LANES = P // PACK
+CHUNKS = SEQ // WIDE
+
+FLOPS = 2 * BATCH * SEQ * (FEAT * CHAN + CHAN * FEAT)
+
+
+def tile_slru_kernel(
+    tc, inputs, Wi_words, Wi_scales, bi, Wo_words, Wo_scales, bo, params_log, out
+):
+    nc = tc.nc
+    with ExitStack() as ctx:
+        keep = ctx.enter_context(tc.tile_pool(name="keep", bufs=1))
+        per_batch = ctx.enter_context(tc.tile_pool(name="per_batch", bufs=BATCH))
+        stream = ctx.enter_context(tc.tile_pool(name="stream", bufs=3))
+        flip_psum = ctx.enter_context(tc.psum_pool(name="flip_psum", bufs=3))
+        sum_psum = ctx.enter_context(tc.psum_pool(name="sum_psum", bufs=5))
+
+        x_rows = keep.tile([P, BATCH * TOK_TILES, FEAT], BF16)
+        x_dram = inputs.rearrange("b (i p) f -> p (b i) f", p=P)
+
+        def load_tokens(first_tile):
+            pair = slice(first_tile, first_tile + 2)
+            nc.sync.dma_start(out=x_rows[:, pair, :], in_=x_dram[:, pair, :])
+
+        w_scales = keep.tile([P, CHAN], U8, align_bytes=64)
+        nc.vector.memset(w_scales[:].bitcast(I32), 0)
+
+        def wi_plane(g):
+            return PACK * g
+
+        def wo_plane(g):
+            return PACK * (PASSES + g)
+
+        def load_weight_scales():
+            for quad in range(4):
+                rows = slice(4 * quad, 4 * quad + 4)
+                for first_plane, scales in ((wi_plane(0), Wi_scales), (wo_plane(0), Wo_scales)):
+                    top = 32 * quad + first_plane
+                    nc.sync.dma_start(
+                        out=w_scales[top : top + PACK * PASSES, :].bitcast(I32),
+                        in_=scales.bitcast(I32)[:, rows, :],
+                    )
+
+        wi_codes = keep.tile([P, PASSES, CHAN], U32, align_bytes=64)
+        wo_codes = keep.tile([P, PASSES, FEAT], U32, align_bytes=64)
+
+        def load_weight_codes(codes, words, half):
+            cols = slice(WIDE * half, WIDE * (half + 1))
+            nc.sync.dma_start(
+                out=codes[:, :, cols].bitcast(I32),
+                in_=words.rearrange("g p n t -> p g (n t)").bitcast(I32)[:, :, cols],
+            )
+
+        load_tokens(0)
+        load_tokens(2)
+        load_weight_scales()
+        load_weight_codes(wi_codes, Wi_words, 0)
+        load_tokens(4)
+        load_tokens(6)
+        load_weight_codes(wi_codes, Wi_words, 1)
+        for first_tile in range(TOK_TILES, BATCH * TOK_TILES, 2):
+            load_tokens(first_tile)
+        load_weight_codes(wo_codes, Wo_words, 0)
+        load_weight_codes(wo_codes, Wo_words, 1)
+
+        ident_f32 = keep.tile([P, P], F32)
+        make_identity(nc, ident_f32[:])
+        ident_bf = keep.tile([P, P], BF16)
+        make_identity(nc, ident_bf[:])
+        sort_bf = keep.tile([P, P], BF16)
+        nc.vector.tensor_copy(
+            out=sort_bf[:].rearrange("k (t c) -> k t c", t=PACK),
+            in_=ident_bf[:].rearrange("k (c t) -> k t c", t=PACK),
+        )
+
+        vec_rows = keep.tile([P, P], BF16)
+        nc.vector.memset(vec_rows[:], 0.0)
+        nc.scalar.dma_start(
+            out=vec_rows[0 : 2 * CHAN_TILES, :],
+            in_=params_log.rearrange("r (j c) -> (r j) c", c=P),
+        )
+        nc.scalar.dma_start(
+            out=vec_rows[2 * CHAN_TILES : 3 * CHAN_TILES, :],
+            in_=bi.rearrange("(j c) -> j c", c=P),
+        )
+        vec_cols = flip_psum.tile([P, P], BF16, tag="flip")
+        nc.tensor.transpose(vec_cols[:], vec_rows[:], ident_bf[:])
+        nu = keep.tile([P, CHAN_TILES], F32)
+        nc.scalar.activation(out=nu[:], in_=vec_cols[:, 0:CHAN_TILES], func=ACT.Exp)
+        decay = keep.tile([P, CHAN_TILES], F32)
+        nc.scalar.activation(out=decay[:], in_=nu[:], func=ACT.Exp, scale=-1.0)
+        gamma = keep.tile([P, CHAN_TILES], F32)
+        nc.scalar.activation(
+            out=gamma[:], in_=vec_cols[:, CHAN_TILES : 2 * CHAN_TILES], func=ACT.Exp
+        )
+        gamma_bi = keep.tile([P, CHAN_TILES], F32)
+        nc.vector.tensor_tensor(
+            out=gamma_bi[:],
+            in0=gamma[:],
+            in1=vec_cols[:, 2 * CHAN_TILES : 3 * CHAN_TILES],
+            op=ALU.mult,
+        )
+
+        bo_row = keep.tile([P, FEAT], BF16)
+        nc.vector.memset(bo_row[:], 0.0)
+        nc.scalar.dma_start(out=bo_row[0:1, :], in_=bo.rearrange("(o f) -> o f", o=1))
+        ones = keep.tile([P, P], BF16)
+        nc.vector.memset(ones[:], 1.0)
+        bo_all = keep.tile([P, FEAT], F32)
+        for half in range(FEAT // WIDE):
+            cols = slice(WIDE * half, WIDE * (half + 1))
+            spread = sum_psum.tile([P, WIDE], F32, tag="sum")
+            nc.tensor.matmul(out=spread[:], lhsT=ones[:], rhs=bo_row[:, cols], start=True, stop=True)
+            nc.vector.tensor_copy(out=bo_all[:, cols], in_=spread[:])
+
+        x_codes = keep.tile([P, PASSES, BATCH * SEQ], U32, align_bytes=64)
+        x_scales = keep.tile([P, PASSES, BATCH * SEQ], U8, align_bytes=64)
+
+        def quantise_inputs(b, chunk):
+            first_tile = b * TOK_TILES + chunk * (WIDE // P)
+            tokens = slice(b * SEQ + chunk * WIDE, b * SEQ + (chunk + 1) * WIDE)
+            for g in range(PASSES):
+                grouped = stream.tile([P, WIDE, PACK], BF16, align_bytes=64, tag="grouped")
+                flat = grouped[:].rearrange("p r t -> p (r t)")
+                halves = flat.bitcast(F32).rearrange("p (r u) -> p r u", u=2)
+                for bank in range(2):
+                    flipped = flip_psum.tile([P, 2, 2 * P], F32, tag="flip")
+                    for i in range(2):
+                        words = x_rows[:, first_tile + 2 * bank + i, :].bitcast(F32)
+                        for u in range(2):
+                            nc.tensor.transpose(
+                                flipped[:, u, P * i : P * (i + 1)],
+                                words[:, 2 * P * g + u : 2 * P * (g + 1) : 2],
+                                ident_f32[:],
+                            )
+                    nc.scalar.copy(
+                        out=halves[:, 2 * P * bank : 2 * P * (bank + 1), :],
+                        in_=flipped[:].rearrange("p u r -> p r u"),
+                    )
+                nc.vector.quantize_mx(
+                    out=x_codes[:, g, tokens].bitcast(FP8X4), scales=x_scales[:, g, tokens], in_=flat
+                )
+
+        def recurrence(b, j):
+            chans = slice(P * j, P * (j + 1))
+            drive = stream.tile([P, SEQ], F32, tag="drive")
+            for chunk in range(CHUNKS):
+                tokens = slice(b * SEQ + chunk * WIDE, b * SEQ + (chunk + 1) * WIDE)
+                acc = sum_psum.tile([P, WIDE], F32, tag="sum")
+                for g in range(PASSES):
+                    nc.tensor.matmul_mx(
+                        out=acc[:],
+                        lhsT=wi_codes[:, g, chans].bitcast(FP8X4),
+                        lhsT_scale=w_scales[wi_plane(g) : P, chans],
+                        rhs=x_codes[:, g, tokens].bitcast(FP8X4),
+                        rhs_scale=x_scales[:, g, tokens],
+                        start=(g == 0),
+                        stop=(g == PASSES - 1),
+                    )
+                nc.scalar.activation(
+                    out=drive[:, WIDE * chunk : WIDE * (chunk + 1)],
+                    in_=acc[:],
+                    func=ACT.Identity,
+                    scale=gamma[:, j : j + 1],
+                    bias=gamma_bi[:, j : j + 1],
+                )
+            x_chan = stream.tile([P, SEQ], BF16, tag="x_chan")
+            nc.vector.tensor_tensor_scan(
+                out=x_chan[:],
+                data0=decay[:, j : j + 1].to_broadcast([P, SEQ]),
+                data1=drive[:],
+                initial=0.0,
+                op0=ALU.mult,
+                op1=ALU.add,
+            )
+            return x_chan
+
+        def to_token_rows(x_chan, x_token, j):
+            g, lane_group = divmod(j, TILES_PER_PASS)
+            lanes = slice(LANES * lane_group, LANES * (lane_group + 1))
+            flipped = flip_psum.tile([P, TOK_TILES, P], BF16, tag="flip")
+            for i in range(TOK_TILES):
+                nc.tensor.transpose(flipped[:, i, :], x_chan[:, P * i : P * (i + 1)], sort_bf[:])
+            nc.scalar.copy(
+                out=x_token[:, :, g, :, lanes],
+                in_=flipped[:].rearrange("p i (t c) -> p i t c", t=PACK),
+            )
+
+        def quantise_x(x_token, s_codes, s_scales, g, chunk):
+            tokens = slice(chunk * WIDE, (chunk + 1) * WIDE)
+            grouped = stream.tile([P, WIDE, PACK], BF16, align_bytes=64, tag="grouped")
+            for bank in range(2):
+                flipped = flip_psum.tile([P, 2, PACK, P], BF16, tag="flip")
+                for i in range(2):
+                    tok_tile = chunk * (WIDE // P) + 2 * bank + i
+                    for t in range(PACK):
+                        nc.tensor.transpose(
+                            flipped[:, i, t, :], x_token[:, tok_tile, g, t, :], ident_bf[:]
+                        )
+                nc.scalar.copy(
+                    out=grouped[:, 2 * P * bank : 2 * P * (bank + 1), :].rearrange(
+                        "p (i r) t -> p i r t", i=2
+                    ),
+                    in_=flipped[:].rearrange("p i t r -> p i r t"),
+                )
+            nc.vector.quantize_mx(
+                out=s_codes[:, g, tokens].bitcast(FP8X4),
+                scales=s_scales[:, g, tokens],
+                in_=grouped[:].rearrange("p r t -> p (r t)"),
+            )
+
+        def second_layer(b, s_codes, s_scales, i):
+            toks = slice(P * i, P * (i + 1))
+            result = stream.tile([P, FEAT], F32, tag="result")
+            for half in range(FEAT // WIDE):
+                cols = slice(WIDE * half, WIDE * (half + 1))
+                acc = sum_psum.tile([P, WIDE], F32, tag="sum")
+                for g in range(PASSES):
+                    nc.tensor.matmul_mx(
+                        out=acc[:],
+                        lhsT=s_codes[:, g, toks].bitcast(FP8X4),
+                        lhsT_scale=s_scales[:, g, toks],
+                        rhs=wo_codes[:, g, cols].bitcast(FP8X4),
+                        rhs_scale=w_scales[wo_plane(g) : P, cols],
+                        start=(g == 0),
+                        stop=(g == PASSES - 1),
+                    )
+                nc.vector.tensor_tensor(
+                    out=result[:, cols], in0=acc[:], in1=bo_all[:, cols], op=ALU.add
+                )
+            nc.sync.dma_start(out=out[b, toks, :], in_=result[:])
+
+        for chunk in range(CHUNKS):
+            quantise_inputs(0, chunk)
+        for b in range(BATCH):
+            x_token = per_batch.tile([P, TOK_TILES, PASSES, PACK, P], BF16, tag="x_token")
+            s_codes = per_batch.tile([P, PASSES, SEQ], U32, align_bytes=64, tag="s_codes")
+            s_scales = per_batch.tile([P, PASSES, SEQ], U8, align_bytes=64, tag="s_scales")
+            for g in range(PASSES):
+                for j in range(TILES_PER_PASS * g, TILES_PER_PASS * (g + 1)):
+                    x_chan = recurrence(b, j)
+                    to_token_rows(x_chan, x_token, j)
+                if b + 1 < BATCH:
+                    quantise_inputs(b + 1, g)
+                for chunk in range(CHUNKS):
+                    quantise_x(x_token, s_codes, s_scales, g, chunk)
+            for i in range(TOK_TILES):
+                second_layer(b, s_codes, s_scales, i)

@@ -24,6 +24,14 @@ CHAN_TILES = CHAN // P
 TILES_PER_PASS = K_PASS // P
 LANES = P // PACK
 CHUNKS = SEQ // WIDE
+PAIR = 2 * P
+PAIRS = SEQ // PAIR
+
+SCANS = BATCH * CHAN_TILES
+AHEAD = 2
+PACK_LAG = 3
+OUT_LAG = 12
+STEPS = BATCH * TOK_TILES + OUT_LAG
 
 FLOPS = 2 * BATCH * SEQ * (FEAT * CHAN + CHAN * FEAT)
 
@@ -33,18 +41,20 @@ def tile_slru_kernel(
 ):
     nc = tc.nc
     with ExitStack() as ctx:
+        ctx.enter_context(tc.manual_schedule())
         keep = ctx.enter_context(tc.tile_pool(name="keep", bufs=1))
         per_batch = ctx.enter_context(tc.tile_pool(name="per_batch", bufs=BATCH))
-        stream = ctx.enter_context(tc.tile_pool(name="stream", bufs=3))
-        flip_psum = ctx.enter_context(tc.psum_pool(name="flip_psum", bufs=3))
-        sum_psum = ctx.enter_context(tc.psum_pool(name="sum_psum", bufs=5))
+        stream = ctx.enter_context(tc.tile_pool(name="stream", bufs=4))
+        flip_psum = ctx.enter_context(tc.psum_pool(name="flip_psum", bufs=2))
+        first_psum = ctx.enter_context(tc.psum_pool(name="first_psum", bufs=3))
+        second_psum = ctx.enter_context(tc.psum_pool(name="second_psum", bufs=3))
 
         x_rows = keep.tile([P, BATCH * TOK_TILES, FEAT], BF16)
         x_dram = inputs.rearrange("b (i p) f -> p (b i) f", p=P)
 
-        def load_tokens(first_tile):
-            pair = slice(first_tile, first_tile + 2)
-            nc.sync.dma_start(out=x_rows[:, pair, :], in_=x_dram[:, pair, :])
+        def load_tokens(pair):
+            tiles = slice(2 * pair, 2 * pair + 2)
+            nc.sync.dma_start(out=x_rows[:, tiles, :], in_=x_dram[:, tiles, :])
 
         w_scales = keep.tile([P, CHAN], U8, align_bytes=64)
         nc.vector.memset(w_scales[:].bitcast(I32), 0)
@@ -55,50 +65,46 @@ def tile_slru_kernel(
         def wo_plane(g):
             return PACK * (PASSES + g)
 
-        def load_weight_scales():
+        def load_weight_scales(scales, first_plane):
             for quad in range(4):
-                rows = slice(4 * quad, 4 * quad + 4)
-                for first_plane, scales in ((wi_plane(0), Wi_scales), (wo_plane(0), Wo_scales)):
-                    top = 32 * quad + first_plane
-                    nc.sync.dma_start(
-                        out=w_scales[top : top + PACK * PASSES, :].bitcast(I32),
-                        in_=scales.bitcast(I32)[:, rows, :],
-                    )
+                top = 32 * quad + first_plane
+                nc.sync.dma_start(
+                    out=w_scales[top : top + PACK * PASSES, :].bitcast(I32),
+                    in_=scales.bitcast(I32)[:, 4 * quad : 4 * quad + 4, :],
+                )
 
         wi_codes = keep.tile([P, PASSES, CHAN], U32, align_bytes=64)
         wo_codes = keep.tile([P, PASSES, FEAT], U32, align_bytes=64)
 
-        def load_weight_codes(codes, words, half):
-            cols = slice(WIDE * half, WIDE * (half + 1))
+        def load_weight_codes(codes, words, first_col, n_cols):
+            cols = slice(first_col, first_col + n_cols)
             nc.sync.dma_start(
                 out=codes[:, :, cols].bitcast(I32),
                 in_=words.rearrange("g p n t -> p g (n t)").bitcast(I32)[:, :, cols],
             )
 
-        load_tokens(0)
-        load_tokens(2)
-        load_weight_scales()
-        load_weight_codes(wi_codes, Wi_words, 0)
-        load_tokens(4)
-        load_tokens(6)
-        load_weight_codes(wi_codes, Wi_words, 1)
-        for first_tile in range(TOK_TILES, BATCH * TOK_TILES, 2):
-            load_tokens(first_tile)
-        load_weight_codes(wo_codes, Wo_words, 0)
-        load_weight_codes(wo_codes, Wo_words, 1)
+        for pair in range(PAIRS):
+            load_tokens(pair)
+        load_weight_scales(Wi_scales, wi_plane(0))
+        for first_col in range(0, CHAN, PAIR):
+            load_weight_codes(wi_codes, Wi_words, first_col, PAIR)
+        for pair in range(PAIRS, BATCH * PAIRS):
+            load_tokens(pair)
+        load_weight_scales(Wo_scales, wo_plane(0))
+        for first_col in range(0, FEAT, WIDE):
+            load_weight_codes(wo_codes, Wo_words, first_col, WIDE)
 
         ident_f32 = keep.tile([P, P], F32)
         make_identity(nc, ident_f32[:])
         ident_bf = keep.tile([P, P], BF16)
         make_identity(nc, ident_bf[:])
-        sort_bf = keep.tile([P, P], BF16)
-        nc.vector.tensor_copy(
-            out=sort_bf[:].rearrange("k (t c) -> k t c", t=PACK),
-            in_=ident_bf[:].rearrange("k (c t) -> k t c", t=PACK),
-        )
 
         vec_rows = keep.tile([P, P], BF16)
         nc.vector.memset(vec_rows[:], 0.0)
+        bo_row = keep.tile([P, FEAT], BF16)
+        nc.vector.memset(bo_row[:], 0.0)
+        ones = keep.tile([P, P], BF16)
+        nc.vector.memset(ones[:], 1.0)
         nc.scalar.dma_start(
             out=vec_rows[0 : 2 * CHAN_TILES, :],
             in_=params_log.rearrange("r (j c) -> (r j) c", c=P),
@@ -107,6 +113,8 @@ def tile_slru_kernel(
             out=vec_rows[2 * CHAN_TILES : 3 * CHAN_TILES, :],
             in_=bi.rearrange("(j c) -> j c", c=P),
         )
+        nc.scalar.dma_start(out=bo_row[0:1, :], in_=bo.rearrange("(o f) -> o f", o=1))
+
         vec_cols = flip_psum.tile([P, P], BF16, tag="flip")
         nc.tensor.transpose(vec_cols[:], vec_rows[:], ident_bf[:])
         nu = keep.tile([P, CHAN_TILES], F32)
@@ -125,52 +133,49 @@ def tile_slru_kernel(
             op=ALU.mult,
         )
 
-        bo_row = keep.tile([P, FEAT], BF16)
-        nc.vector.memset(bo_row[:], 0.0)
-        nc.scalar.dma_start(out=bo_row[0:1, :], in_=bo.rearrange("(o f) -> o f", o=1))
-        ones = keep.tile([P, P], BF16)
-        nc.vector.memset(ones[:], 1.0)
         bo_all = keep.tile([P, FEAT], F32)
-        for half in range(FEAT // WIDE):
-            cols = slice(WIDE * half, WIDE * (half + 1))
-            spread = sum_psum.tile([P, WIDE], F32, tag="sum")
-            nc.tensor.matmul(out=spread[:], lhsT=ones[:], rhs=bo_row[:, cols], start=True, stop=True)
-            nc.vector.tensor_copy(out=bo_all[:, cols], in_=spread[:])
+
+        def spread_bo():
+            for half in range(FEAT // WIDE):
+                cols = slice(WIDE * half, WIDE * (half + 1))
+                spread = second_psum.tile([P, WIDE], F32, tag="second")
+                nc.tensor.matmul(
+                    out=spread[:], lhsT=ones[:], rhs=bo_row[:, cols], start=True, stop=True
+                )
+                nc.vector.tensor_copy(out=bo_all[:, cols], in_=spread[:])
 
         x_codes = keep.tile([P, PASSES, BATCH * SEQ], U32, align_bytes=64)
         x_scales = keep.tile([P, PASSES, BATCH * SEQ], U8, align_bytes=64)
 
-        def quantise_inputs(b, chunk):
-            first_tile = b * TOK_TILES + chunk * (WIDE // P)
-            tokens = slice(b * SEQ + chunk * WIDE, b * SEQ + (chunk + 1) * WIDE)
+        def quantise_inputs(pair):
+            tokens = slice(PAIR * pair, PAIR * (pair + 1))
             for g in range(PASSES):
-                grouped = stream.tile([P, WIDE, PACK], BF16, align_bytes=64, tag="grouped")
-                flat = grouped[:].rearrange("p r t -> p (r t)")
-                halves = flat.bitcast(F32).rearrange("p (r u) -> p r u", u=2)
-                for bank in range(2):
-                    flipped = flip_psum.tile([P, 2, 2 * P], F32, tag="flip")
-                    for i in range(2):
-                        words = x_rows[:, first_tile + 2 * bank + i, :].bitcast(F32)
-                        for u in range(2):
-                            nc.tensor.transpose(
-                                flipped[:, u, P * i : P * (i + 1)],
-                                words[:, 2 * P * g + u : 2 * P * (g + 1) : 2],
-                                ident_f32[:],
-                            )
-                    nc.scalar.copy(
-                        out=halves[:, 2 * P * bank : 2 * P * (bank + 1), :],
-                        in_=flipped[:].rearrange("p u r -> p r u"),
-                    )
+                flipped = flip_psum.tile([P, 2, PAIR], F32, tag="flip")
+                for i in range(2):
+                    words = x_rows[:, 2 * pair + i, :].bitcast(F32)
+                    for u in range(2):
+                        nc.tensor.transpose(
+                            flipped[:, u, P * i : P * (i + 1)],
+                            words[:, 2 * P * g + u : 2 * P * (g + 1) : 2],
+                            ident_f32[:],
+                        )
+                grouped = stream.tile([P, PAIR * PACK], BF16, align_bytes=64, tag="grouped_in")
+                nc.scalar.copy(
+                    out=grouped[:].bitcast(F32).rearrange("p (r u) -> p r u", u=2),
+                    in_=flipped[:].rearrange("p u r -> p r u"),
+                )
                 nc.vector.quantize_mx(
-                    out=x_codes[:, g, tokens].bitcast(FP8X4), scales=x_scales[:, g, tokens], in_=flat
+                    out=x_codes[:, g, tokens].bitcast(FP8X4),
+                    scales=x_scales[:, g, tokens],
+                    in_=grouped[:],
                 )
 
-        def recurrence(b, j):
+        def first_layer(b, j):
             chans = slice(P * j, P * (j + 1))
             drive = stream.tile([P, SEQ], F32, tag="drive")
             for chunk in range(CHUNKS):
                 tokens = slice(b * SEQ + chunk * WIDE, b * SEQ + (chunk + 1) * WIDE)
-                acc = sum_psum.tile([P, WIDE], F32, tag="sum")
+                acc = first_psum.tile([P, WIDE], F32, tag="first")
                 for g in range(PASSES):
                     nc.tensor.matmul_mx(
                         out=acc[:],
@@ -188,6 +193,9 @@ def tile_slru_kernel(
                     scale=gamma[:, j : j + 1],
                     bias=gamma_bi[:, j : j + 1],
                 )
+            return drive
+
+        def recurrence(drive, x_lanes, j):
             x_chan = stream.tile([P, SEQ], BF16, tag="x_chan")
             nc.vector.tensor_tensor_scan(
                 out=x_chan[:],
@@ -197,36 +205,18 @@ def tile_slru_kernel(
                 op0=ALU.mult,
                 op1=ALU.add,
             )
-            return x_chan
-
-        def to_token_rows(x_chan, x_token, j):
             g, lane_group = divmod(j, TILES_PER_PASS)
             lanes = slice(LANES * lane_group, LANES * (lane_group + 1))
-            flipped = flip_psum.tile([P, TOK_TILES, P], BF16, tag="flip")
-            for i in range(TOK_TILES):
-                nc.tensor.transpose(flipped[:, i, :], x_chan[:, P * i : P * (i + 1)], sort_bf[:])
-            nc.scalar.copy(
-                out=x_token[:, :, g, :, lanes],
-                in_=flipped[:].rearrange("p i (t c) -> p i t c", t=PACK),
-            )
+            for t in range(PACK):
+                nc.sync.dma_start(out=x_lanes[lanes, g, t, :], in_=x_chan[t:P:PACK, :])
 
-        def quantise_x(x_token, s_codes, s_scales, g, chunk):
+        def quantise_x(x_lanes, s_codes, s_scales, g, chunk):
             tokens = slice(chunk * WIDE, (chunk + 1) * WIDE)
-            grouped = stream.tile([P, WIDE, PACK], BF16, align_bytes=64, tag="grouped")
-            for bank in range(2):
-                flipped = flip_psum.tile([P, 2, PACK, P], BF16, tag="flip")
-                for i in range(2):
-                    tok_tile = chunk * (WIDE // P) + 2 * bank + i
-                    for t in range(PACK):
-                        nc.tensor.transpose(
-                            flipped[:, i, t, :], x_token[:, tok_tile, g, t, :], ident_bf[:]
-                        )
-                nc.scalar.copy(
-                    out=grouped[:, 2 * P * bank : 2 * P * (bank + 1), :].rearrange(
-                        "p (i r) t -> p i r t", i=2
-                    ),
-                    in_=flipped[:].rearrange("p i t r -> p i r t"),
-                )
+            grouped = stream.tile([P, WIDE, PACK], BF16, align_bytes=64, tag="grouped_x")
+            nc.scalar.copy(
+                out=grouped[:].rearrange("p (c i) t -> p c t i", i=4),
+                in_=x_lanes[:, g, :, tokens].rearrange("p t (c i) -> p c t i", i=4),
+            )
             nc.vector.quantize_mx(
                 out=s_codes[:, g, tokens].bitcast(FP8X4),
                 scales=s_scales[:, g, tokens],
@@ -238,7 +228,7 @@ def tile_slru_kernel(
             result = stream.tile([P, FEAT], F32, tag="result")
             for half in range(FEAT // WIDE):
                 cols = slice(WIDE * half, WIDE * (half + 1))
-                acc = sum_psum.tile([P, WIDE], F32, tag="sum")
+                acc = second_psum.tile([P, WIDE], F32, tag="second")
                 for g in range(PASSES):
                     nc.tensor.matmul_mx(
                         out=acc[:],
@@ -254,19 +244,44 @@ def tile_slru_kernel(
                 )
             nc.sync.dma_start(out=out[b, toks, :], in_=result[:])
 
-        for chunk in range(CHUNKS):
-            quantise_inputs(0, chunk)
-        for b in range(BATCH):
-            x_token = per_batch.tile([P, TOK_TILES, PASSES, PACK, P], BF16, tag="x_token")
-            s_codes = per_batch.tile([P, PASSES, SEQ], U32, align_bytes=64, tag="s_codes")
-            s_scales = per_batch.tile([P, PASSES, SEQ], U8, align_bytes=64, tag="s_scales")
-            for g in range(PASSES):
-                for j in range(TILES_PER_PASS * g, TILES_PER_PASS * (g + 1)):
-                    x_chan = recurrence(b, j)
-                    to_token_rows(x_chan, x_token, j)
-                if b + 1 < BATCH:
-                    quantise_inputs(b + 1, g)
-                for chunk in range(CHUNKS):
-                    quantise_x(x_token, s_codes, s_scales, g, chunk)
-            for i in range(TOK_TILES):
-                second_layer(b, s_codes, s_scales, i)
+        x_lanes = [
+            per_batch.tile([P, PASSES, PACK, SEQ], BF16, name="x_lanes%d" % b, tag="x_lanes")
+            for b in range(BATCH)
+        ]
+        s_codes = [
+            per_batch.tile(
+                [P, PASSES, SEQ], U32, align_bytes=64, name="s_codes%d" % b, tag="s_codes"
+            )
+            for b in range(BATCH)
+        ]
+        s_scales = [
+            per_batch.tile(
+                [P, PASSES, SEQ], U8, align_bytes=64, name="s_scales%d" % b, tag="s_scales"
+            )
+            for b in range(BATCH)
+        ]
+        drives = {}
+
+        quantise_inputs(0)
+        spread_bo()
+        for pair in range(1, PAIRS):
+            quantise_inputs(pair)
+        for k in range(AHEAD):
+            drives[k] = first_layer(0, k)
+
+        for k in range(STEPS):
+            if k + AHEAD < SCANS:
+                b, j = divmod(k + AHEAD, CHAN_TILES)
+                drives[k + AHEAD] = first_layer(b, j)
+            if k < SCANS:
+                b, j = divmod(k, CHAN_TILES)
+                recurrence(drives[k], x_lanes[b], j)
+            if k < (BATCH - 1) * PAIRS:
+                quantise_inputs(PAIRS + k)
+            if 0 <= k - OUT_LAG:
+                b, i = divmod(k - OUT_LAG, TOK_TILES)
+                second_layer(b, s_codes[b], s_scales[b], i)
+            n, chunk = divmod(k - (TILES_PER_PASS - 1) - PACK_LAG, TILES_PER_PASS)
+            if 0 <= n < BATCH * PASSES and chunk < CHUNKS:
+                b, g = divmod(n, PASSES)
+                quantise_x(x_lanes[b], s_codes[b], s_scales[b], g, chunk)

@@ -29,6 +29,7 @@ PAIRS = SEQ // PAIR
 
 SCANS = BATCH * CHAN_TILES
 AHEAD = 2
+IN_LAG = 1
 PACK_LAG = 3
 OUT_LAG = 12
 STEPS = BATCH * TOK_TILES + OUT_LAG
@@ -48,6 +49,24 @@ def tile_slru_kernel(
         flip_psum = ctx.enter_context(tc.psum_pool(name="flip_psum", bufs=2))
         first_psum = ctx.enter_context(tc.psum_pool(name="first_psum", bufs=3))
         second_psum = ctx.enter_context(tc.psum_pool(name="second_psum", bufs=3))
+
+        vec_rows = keep.tile([P, P], BF16)
+        nc.vector.memset(vec_rows[:], 0.0)
+        bo_row = keep.tile([P, FEAT], BF16)
+        nc.vector.memset(bo_row[:], 0.0)
+        ones = keep.tile([P, P], BF16)
+        nc.vector.memset(ones[:], 1.0)
+        nc.scalar.dma_start(
+            out=vec_rows[0 : 2 * CHAN_TILES, :],
+            in_=params_log.rearrange("r (j c) -> (r j) c", c=P),
+        )
+        nc.scalar.dma_start(
+            out=vec_rows[2 * CHAN_TILES : 3 * CHAN_TILES, :],
+            in_=bi.rearrange("(j c) -> j c", c=P),
+        )
+        nc.scalar.dma_start(out=bo_row[0:1, :], in_=bo.rearrange("(o f) -> o f", o=1))
+        warm = keep.tile([P, 1], F32)
+        nc.scalar.activation(out=warm[:], in_=ones[:, 0:1], func=ACT.Exp)
 
         x_rows = keep.tile([P, BATCH * TOK_TILES, FEAT], BF16)
         x_dram = inputs.rearrange("b (i p) f -> p (b i) f", p=P)
@@ -99,23 +118,7 @@ def tile_slru_kernel(
         ident_bf = keep.tile([P, P], BF16)
         make_identity(nc, ident_bf[:])
 
-        vec_rows = keep.tile([P, P], BF16)
-        nc.vector.memset(vec_rows[:], 0.0)
-        bo_row = keep.tile([P, FEAT], BF16)
-        nc.vector.memset(bo_row[:], 0.0)
-        ones = keep.tile([P, P], BF16)
-        nc.vector.memset(ones[:], 1.0)
-        nc.scalar.dma_start(
-            out=vec_rows[0 : 2 * CHAN_TILES, :],
-            in_=params_log.rearrange("r (j c) -> (r j) c", c=P),
-        )
-        nc.scalar.dma_start(
-            out=vec_rows[2 * CHAN_TILES : 3 * CHAN_TILES, :],
-            in_=bi.rearrange("(j c) -> j c", c=P),
-        )
-        nc.scalar.dma_start(out=bo_row[0:1, :], in_=bo.rearrange("(o f) -> o f", o=1))
-
-        vec_cols = flip_psum.tile([P, P], BF16, tag="flip")
+        vec_cols = second_psum.tile([P, P], BF16, tag="second")
         nc.tensor.transpose(vec_cols[:], vec_rows[:], ident_bf[:])
         nu = keep.tile([P, CHAN_TILES], F32)
         nc.scalar.activation(out=nu[:], in_=vec_cols[:, 0:CHAN_TILES], func=ACT.Exp)
@@ -142,7 +145,7 @@ def tile_slru_kernel(
                 nc.tensor.matmul(
                     out=spread[:], lhsT=ones[:], rhs=bo_row[:, cols], start=True, stop=True
                 )
-                nc.vector.tensor_copy(out=bo_all[:, cols], in_=spread[:])
+                nc.scalar.copy(out=bo_all[:, cols], in_=spread[:])
 
         x_codes = keep.tile([P, PASSES, BATCH * SEQ], U32, align_bytes=64)
         x_scales = keep.tile([P, PASSES, BATCH * SEQ], U8, align_bytes=64)
@@ -262,12 +265,11 @@ def tile_slru_kernel(
         ]
         drives = {}
 
-        quantise_inputs(0)
-        spread_bo()
-        for pair in range(1, PAIRS):
+        for pair in range(PAIRS):
             quantise_inputs(pair)
         for k in range(AHEAD):
             drives[k] = first_layer(0, k)
+        spread_bo()
 
         for k in range(STEPS):
             if k + AHEAD < SCANS:
@@ -276,8 +278,8 @@ def tile_slru_kernel(
             if k < SCANS:
                 b, j = divmod(k, CHAN_TILES)
                 recurrence(drives[k], x_lanes[b], j)
-            if k < (BATCH - 1) * PAIRS:
-                quantise_inputs(PAIRS + k)
+            if 0 <= k - IN_LAG < (BATCH - 1) * PAIRS:
+                quantise_inputs(PAIRS + k - IN_LAG)
             if 0 <= k - OUT_LAG:
                 b, i = divmod(k - OUT_LAG, TOK_TILES)
                 second_layer(b, s_codes[b], s_scales[b], i)

@@ -19,20 +19,21 @@ PACK = 4
 K_PASS = P * PACK
 PASSES = FEAT // K_PASS
 WIDE = 512
-TOK_TILES = SEQ // P
 CHAN_TILES = CHAN // P
-TILES_PER_PASS = K_PASS // P
-LANES = P // PACK
-CHUNKS = SEQ // WIDE
 PAIR = 2 * P
-PAIRS = SEQ // PAIR
+CHUNK = WIDE
+CHUNKS = BATCH * SEQ // CHUNK
+CHUNKS_PER_SEQ = SEQ // CHUNK
+UNITS = CHUNK // PAIR * PASSES
+HALVES = 2
+HALF = CHUNK // HALVES
+OUT_UNITS = (CHUNK // P) * (FEAT // WIDE)
 
-SCANS = BATCH * CHAN_TILES
+SCANS = CHUNKS * CHAN_TILES
 AHEAD = 2
-IN_LAG = 1
-PACK_LAG = 3
-OUT_LAG = 12
-STEPS = BATCH * TOK_TILES + OUT_LAG
+MM2_LAG = 9
+ADD_LAG = 10
+STEPS = SCANS + ADD_LAG
 
 FLOPS = 2 * BATCH * SEQ * (FEAT * CHAN + CHAN * FEAT)
 
@@ -44,55 +45,51 @@ def tile_slru_kernel(
     with ExitStack() as ctx:
         ctx.enter_context(tc.manual_schedule())
         keep = ctx.enter_context(tc.tile_pool(name="keep", bufs=1))
-        per_batch = ctx.enter_context(tc.tile_pool(name="per_batch", bufs=BATCH))
         stream = ctx.enter_context(tc.tile_pool(name="stream", bufs=4))
         flip_psum = ctx.enter_context(tc.psum_pool(name="flip_psum", bufs=2))
         first_psum = ctx.enter_context(tc.psum_pool(name="first_psum", bufs=3))
         second_psum = ctx.enter_context(tc.psum_pool(name="second_psum", bufs=3))
 
-        vec_rows = keep.tile([P, P], BF16)
-        nc.vector.memset(vec_rows[:], 0.0)
-        bo_row = keep.tile([P, FEAT], BF16)
-        nc.vector.memset(bo_row[:], 0.0)
-        ones = keep.tile([P, P], BF16)
-        nc.vector.memset(ones[:], 1.0)
+        par = keep.tile([P, 3 * PASSES, PACK], BF16)
         nc.scalar.dma_start(
-            out=vec_rows[0 : 2 * CHAN_TILES, :],
-            in_=params_log.rearrange("r (j c) -> (r j) c", c=P),
+            out=par[:, 0 : 2 * PASSES, :],
+            in_=params_log.rearrange("r (g p t) -> p (r g) t", p=P, t=PACK),
         )
         nc.scalar.dma_start(
-            out=vec_rows[2 * CHAN_TILES : 3 * CHAN_TILES, :],
-            in_=bi.rearrange("(j c) -> j c", c=P),
+            out=par[:, 2 * PASSES : 3 * PASSES, :],
+            in_=bi.rearrange("(g p t) -> p g t", p=P, t=PACK),
         )
-        nc.scalar.dma_start(out=bo_row[0:1, :], in_=bo.rearrange("(o f) -> o f", o=1))
+        zero = keep.tile([P, 1], F32)
+        nc.vector.memset(zero[:], 0.0)
         warm = keep.tile([P, 1], F32)
-        nc.scalar.activation(out=warm[:], in_=ones[:, 0:1], func=ACT.Exp)
+        nc.scalar.activation(out=warm[:], in_=zero[:], func=ACT.Exp)
 
-        x_rows = keep.tile([P, BATCH * TOK_TILES, FEAT], BF16)
+        wi_sc_raw = keep.tile([P, CHAN], U8, align_bytes=64)
+        nc.vector.memset(wi_sc_raw[:].bitcast(I32), 0)
+        wo_sc = keep.tile([P, FEAT], U8, align_bytes=64)
+        nc.vector.memset(wo_sc[:].bitcast(I32), 0)
+
+        def plane(g):
+            return PACK * g
+
+        def load_weight_scales(planes, scales):
+            for quad in range(4):
+                top = 32 * quad
+                nc.sync.dma_start(
+                    out=planes[top : top + PACK * PASSES, :].bitcast(I32),
+                    in_=scales.bitcast(I32)[:, 4 * quad : 4 * quad + 4, :],
+                )
+
+        x_rows = keep.tile([P, BATCH * SEQ // P, FEAT], BF16)
         x_dram = inputs.rearrange("b (i p) f -> p (b i) f", p=P)
 
         def load_tokens(pair):
             tiles = slice(2 * pair, 2 * pair + 2)
             nc.sync.dma_start(out=x_rows[:, tiles, :], in_=x_dram[:, tiles, :])
 
-        w_scales = keep.tile([P, CHAN], U8, align_bytes=64)
-        nc.vector.memset(w_scales[:].bitcast(I32), 0)
-
-        def wi_plane(g):
-            return PACK * g
-
-        def wo_plane(g):
-            return PACK * (PASSES + g)
-
-        def load_weight_scales(scales, first_plane):
-            for quad in range(4):
-                top = 32 * quad + first_plane
-                nc.sync.dma_start(
-                    out=w_scales[top : top + PACK * PASSES, :].bitcast(I32),
-                    in_=scales.bitcast(I32)[:, 4 * quad : 4 * quad + 4, :],
-                )
-
+        wi_raw = keep.tile([P, PASSES, CHAN], U32, align_bytes=64)
         wi_codes = keep.tile([P, PASSES, CHAN], U32, align_bytes=64)
+        wi_sc = keep.tile([P, CHAN], U8, align_bytes=64)
         wo_codes = keep.tile([P, PASSES, FEAT], U32, align_bytes=64)
 
         def load_weight_codes(codes, words, first_col, n_cols):
@@ -102,188 +99,216 @@ def tile_slru_kernel(
                 in_=words.rearrange("g p n t -> p g (n t)").bitcast(I32)[:, :, cols],
             )
 
-        for pair in range(PAIRS):
+        load_weight_scales(wi_sc_raw, Wi_scales)
+        load_weight_scales(wo_sc, Wo_scales)
+        load_weight_codes(wi_raw, Wi_words, 0, K_PASS)
+        load_weight_codes(wi_raw, Wi_words, K_PASS, K_PASS)
+        for pair in range(BATCH * SEQ // PAIR):
             load_tokens(pair)
-        load_weight_scales(Wi_scales, wi_plane(0))
-        for first_col in range(0, CHAN, PAIR):
-            load_weight_codes(wi_codes, Wi_words, first_col, PAIR)
-        for pair in range(PAIRS, BATCH * PAIRS):
-            load_tokens(pair)
-        load_weight_scales(Wo_scales, wo_plane(0))
         for first_col in range(0, FEAT, WIDE):
             load_weight_codes(wo_codes, Wo_words, first_col, WIDE)
+        bo_all = keep.tile([P, FEAT], BF16)
+        nc.sync.dma_start(out=bo_all[:], in_=bo.partition_broadcast(P))
 
         ident_f32 = keep.tile([P, P], F32)
         make_identity(nc, ident_f32[:])
-        ident_bf = keep.tile([P, P], BF16)
-        make_identity(nc, ident_bf[:])
 
-        vec_cols = second_psum.tile([P, P], BF16, tag="second")
-        nc.tensor.transpose(vec_cols[:], vec_rows[:], ident_bf[:])
         nu = keep.tile([P, CHAN_TILES], F32)
-        nc.scalar.activation(out=nu[:], in_=vec_cols[:, 0:CHAN_TILES], func=ACT.Exp)
+        nc.scalar.activation(
+            out=nu[:], in_=par[:, 0:PASSES, :].rearrange("p g t -> p (g t)"), func=ACT.Exp
+        )
         decay = keep.tile([P, CHAN_TILES], F32)
         nc.scalar.activation(out=decay[:], in_=nu[:], func=ACT.Exp, scale=-1.0)
         gamma = keep.tile([P, CHAN_TILES], F32)
         nc.scalar.activation(
-            out=gamma[:], in_=vec_cols[:, CHAN_TILES : 2 * CHAN_TILES], func=ACT.Exp
+            out=gamma[:],
+            in_=par[:, PASSES : 2 * PASSES, :].rearrange("p g t -> p (g t)"),
+            func=ACT.Exp,
         )
         gamma_bi = keep.tile([P, CHAN_TILES], F32)
-        nc.vector.tensor_tensor(
+        nc.gpsimd.tensor_tensor(
             out=gamma_bi[:],
             in0=gamma[:],
-            in1=vec_cols[:, 2 * CHAN_TILES : 3 * CHAN_TILES],
+            in1=par[:, 2 * PASSES : 3 * PASSES, :].rearrange("p g t -> p (g t)"),
             op=ALU.mult,
         )
 
-        bo_all = keep.tile([P, FEAT], F32)
-
-        def spread_bo():
-            for half in range(FEAT // WIDE):
-                cols = slice(WIDE * half, WIDE * (half + 1))
-                spread = second_psum.tile([P, WIDE], F32, tag="second")
-                nc.tensor.matmul(
-                    out=spread[:], lhsT=ones[:], rhs=bo_row[:, cols], start=True, stop=True
-                )
-                nc.scalar.copy(out=bo_all[:, cols], in_=spread[:])
+        def permute_wi(grp):
+            cols = slice(K_PASS * grp, K_PASS * (grp + 1))
+            nc.vector.tensor_copy(
+                out=wi_sc[:, cols].rearrange("p (t m) -> p m t", t=PACK),
+                in_=wi_sc_raw[:, cols].rearrange("p (m t) -> p m t", t=PACK),
+            )
+            nc.vector.tensor_copy(
+                out=wi_codes[:].bitcast(I32)[:, :, cols].rearrange("p g (t m) -> p g t m", t=PACK),
+                in_=wi_raw[:].bitcast(I32)[:, :, cols].rearrange("p g (m t) -> p g t m", t=PACK),
+            )
 
         x_codes = keep.tile([P, PASSES, BATCH * SEQ], U32, align_bytes=64)
         x_scales = keep.tile([P, PASSES, BATCH * SEQ], U8, align_bytes=64)
+        grouped_in = {}
 
-        def quantise_inputs(pair):
-            tokens = slice(PAIR * pair, PAIR * (pair + 1))
-            for g in range(PASSES):
-                flipped = flip_psum.tile([P, 2, PAIR], F32, tag="flip")
-                for i in range(2):
-                    words = x_rows[:, 2 * pair + i, :].bitcast(F32)
-                    for u in range(2):
-                        nc.tensor.transpose(
-                            flipped[:, u, P * i : P * (i + 1)],
-                            words[:, 2 * P * g + u : 2 * P * (g + 1) : 2],
-                            ident_f32[:],
-                        )
-                grouped = stream.tile([P, PAIR * PACK], BF16, align_bytes=64, tag="grouped_in")
-                nc.scalar.copy(
-                    out=grouped[:].bitcast(F32).rearrange("p (r u) -> p r u", u=2),
-                    in_=flipped[:].rearrange("p u r -> p r u"),
-                )
-                nc.vector.quantize_mx(
-                    out=x_codes[:, g, tokens].bitcast(FP8X4),
-                    scales=x_scales[:, g, tokens],
-                    in_=grouped[:],
-                )
-
-        def first_layer(b, j):
-            chans = slice(P * j, P * (j + 1))
-            drive = stream.tile([P, SEQ], F32, tag="drive")
-            for chunk in range(CHUNKS):
-                tokens = slice(b * SEQ + chunk * WIDE, b * SEQ + (chunk + 1) * WIDE)
-                acc = first_psum.tile([P, WIDE], F32, tag="first")
-                for g in range(PASSES):
-                    nc.tensor.matmul_mx(
-                        out=acc[:],
-                        lhsT=wi_codes[:, g, chans].bitcast(FP8X4),
-                        lhsT_scale=w_scales[wi_plane(g) : P, chans],
-                        rhs=x_codes[:, g, tokens].bitcast(FP8X4),
-                        rhs_scale=x_scales[:, g, tokens],
-                        start=(g == 0),
-                        stop=(g == PASSES - 1),
+        def flip_inputs(unit):
+            pair, g = divmod(unit, PASSES)
+            flipped = flip_psum.tile([P, 2, PAIR], F32, tag="flip")
+            for i in range(2):
+                words = x_rows[:, 2 * pair + i, :].bitcast(F32)
+                for u in range(2):
+                    nc.tensor.transpose(
+                        flipped[:, u, P * i : P * (i + 1)],
+                        words[:, 2 * P * g + u : 2 * P * (g + 1) : 2],
+                        ident_f32[:],
                     )
-                nc.scalar.activation(
-                    out=drive[:, WIDE * chunk : WIDE * (chunk + 1)],
-                    in_=acc[:],
-                    func=ACT.Identity,
-                    scale=gamma[:, j : j + 1],
-                    bias=gamma_bi[:, j : j + 1],
-                )
-            return drive
+            grouped = stream.tile([P, PAIR * PACK], BF16, align_bytes=64, tag="grouped_in")
+            nc.scalar.copy(
+                out=grouped[:].bitcast(F32).rearrange("p (r u) -> p r u", u=2),
+                in_=flipped[:].rearrange("p u r -> p r u"),
+            )
+            grouped_in[unit] = grouped
 
-        def recurrence(drive, x_lanes, j):
-            x_chan = stream.tile([P, SEQ], BF16, tag="x_chan")
+        def quantise_inputs(unit):
+            pair, g = divmod(unit, PASSES)
+            tokens = slice(PAIR * pair, PAIR * (pair + 1))
+            nc.vector.quantize_mx(
+                out=x_codes[:, g, tokens].bitcast(FP8X4),
+                scales=x_scales[:, g, tokens],
+                in_=grouped_in[unit][:],
+            )
+
+        drives = {}
+
+        def first_layer(k):
+            q, j = divmod(k, CHAN_TILES)
+            chans = slice(P * j, P * (j + 1))
+            tokens = slice(q * CHUNK, (q + 1) * CHUNK)
+            acc = first_psum.tile([P, WIDE], F32, tag="first")
+            for g in range(PASSES):
+                nc.tensor.matmul_mx(
+                    out=acc[:],
+                    lhsT=wi_codes[:, g, chans].bitcast(FP8X4),
+                    lhsT_scale=wi_sc[plane(g) : P, chans],
+                    rhs=x_codes[:, g, tokens].bitcast(FP8X4),
+                    rhs_scale=x_scales[:, g, tokens],
+                    start=(g == 0),
+                    stop=(g == PASSES - 1),
+                )
+            drive = stream.tile([P, CHUNK], F32, tag="drive")
+            nc.scalar.activation(
+                out=drive[:],
+                in_=acc[:],
+                func=ACT.Identity,
+                scale=gamma[:, j : j + 1],
+                bias=gamma_bi[:, j : j + 1],
+            )
+            drives[k] = drive
+
+        states = {}
+
+        def recurrence(k):
+            q, j = divmod(k, CHAN_TILES)
+            grp, t = divmod(j, PACK)
+            if t == 0:
+                states[(q, grp)] = stream.tile(
+                    [P, PACK, CHUNK], F32, name="state%d_%d" % (q, grp), tag="state"
+                )
+            if q % CHUNKS_PER_SEQ == 0:
+                carry = 0.0
+            else:
+                carry = states[(q - 1, grp)][:, t, CHUNK - 1 : CHUNK]
             nc.vector.tensor_tensor_scan(
-                out=x_chan[:],
-                data0=decay[:, j : j + 1].to_broadcast([P, SEQ]),
-                data1=drive[:],
-                initial=0.0,
+                out=states[(q, grp)][:, t, :],
+                data0=decay[:, j : j + 1].to_broadcast([P, CHUNK]),
+                data1=drives[k][:],
+                initial=carry,
                 op0=ALU.mult,
                 op1=ALU.add,
             )
-            g, lane_group = divmod(j, TILES_PER_PASS)
-            lanes = slice(LANES * lane_group, LANES * (lane_group + 1))
-            for t in range(PACK):
-                nc.sync.dma_start(out=x_lanes[lanes, g, t, :], in_=x_chan[t:P:PACK, :])
 
-        def quantise_x(x_lanes, s_codes, s_scales, g, chunk):
-            tokens = slice(chunk * WIDE, (chunk + 1) * WIDE)
-            grouped = stream.tile([P, WIDE, PACK], BF16, align_bytes=64, tag="grouped_x")
+        s_codes = keep.tile([P, PASSES, BATCH * SEQ], U32, align_bytes=64)
+        s_scales = keep.tile([P, PASSES, BATCH * SEQ], U8, align_bytes=64)
+        grouped_x = {}
+
+        def interleave_x(q, grp, piece):
+            local = slice(piece * HALF, (piece + 1) * HALF)
+            grouped = stream.tile([P, HALF, PACK], BF16, align_bytes=64, tag="grouped_x")
             nc.scalar.copy(
                 out=grouped[:].rearrange("p (c i) t -> p c t i", i=4),
-                in_=x_lanes[:, g, :, tokens].rearrange("p t (c i) -> p c t i", i=4),
+                in_=states[(q, grp)][:, :, local].rearrange("p t (c i) -> p c t i", i=4),
             )
+            grouped_x[(q, grp, piece)] = grouped
+
+        def quantise_x(q, grp, piece):
+            tokens = slice(q * CHUNK + piece * HALF, q * CHUNK + (piece + 1) * HALF)
             nc.vector.quantize_mx(
-                out=s_codes[:, g, tokens].bitcast(FP8X4),
-                scales=s_scales[:, g, tokens],
-                in_=grouped[:].rearrange("p r t -> p (r t)"),
+                out=s_codes[:, grp, tokens].bitcast(FP8X4),
+                scales=s_scales[:, grp, tokens],
+                in_=grouped_x[(q, grp, piece)][:].rearrange("p r t -> p (r t)"),
             )
 
-        def second_layer(b, s_codes, s_scales, i):
+        sums = {}
+        results = {}
+
+        def second_matmul(n):
+            i, half = divmod(n, FEAT // WIDE)
             toks = slice(P * i, P * (i + 1))
-            result = stream.tile([P, FEAT], F32, tag="result")
-            for half in range(FEAT // WIDE):
-                cols = slice(WIDE * half, WIDE * (half + 1))
-                acc = second_psum.tile([P, WIDE], F32, tag="second")
-                for g in range(PASSES):
-                    nc.tensor.matmul_mx(
-                        out=acc[:],
-                        lhsT=s_codes[:, g, toks].bitcast(FP8X4),
-                        lhsT_scale=s_scales[:, g, toks],
-                        rhs=wo_codes[:, g, cols].bitcast(FP8X4),
-                        rhs_scale=w_scales[wo_plane(g) : P, cols],
-                        start=(g == 0),
-                        stop=(g == PASSES - 1),
-                    )
-                nc.vector.tensor_tensor(
-                    out=result[:, cols], in0=acc[:], in1=bo_all[:, cols], op=ALU.add
+            cols = slice(WIDE * half, WIDE * (half + 1))
+            acc = second_psum.tile([P, WIDE], F32, tag="second")
+            for g in range(PASSES):
+                nc.tensor.matmul_mx(
+                    out=acc[:],
+                    lhsT=s_codes[:, g, toks].bitcast(FP8X4),
+                    lhsT_scale=s_scales[:, g, toks],
+                    rhs=wo_codes[:, g, cols].bitcast(FP8X4),
+                    rhs_scale=wo_sc[plane(g) : P, cols],
+                    start=(g == 0),
+                    stop=(g == PASSES - 1),
                 )
-            nc.sync.dma_start(out=out[b, toks, :], in_=result[:])
+            sums[n] = acc
 
-        x_lanes = [
-            per_batch.tile([P, PASSES, PACK, SEQ], BF16, name="x_lanes%d" % b, tag="x_lanes")
-            for b in range(BATCH)
-        ]
-        s_codes = [
-            per_batch.tile(
-                [P, PASSES, SEQ], U32, align_bytes=64, name="s_codes%d" % b, tag="s_codes"
-            )
-            for b in range(BATCH)
-        ]
-        s_scales = [
-            per_batch.tile(
-                [P, PASSES, SEQ], U8, align_bytes=64, name="s_scales%d" % b, tag="s_scales"
-            )
-            for b in range(BATCH)
-        ]
-        drives = {}
+        out_rows = out.rearrange("b s f -> (b s) f")
 
-        for pair in range(PAIRS):
-            quantise_inputs(pair)
+        def add_bias(n):
+            i, half = divmod(n, FEAT // WIDE)
+            cols = slice(WIDE * half, WIDE * (half + 1))
+            if half == 0:
+                results[i] = stream.tile([P, FEAT], F32, name="result%d" % i, tag="result")
+            nc.vector.tensor_tensor(
+                out=results[i][:, cols], in0=sums[n][:], in1=bo_all[:, cols], op=ALU.add
+            )
+            if half == FEAT // WIDE - 1:
+                nc.sync.dma_start(out=out_rows[P * i : P * (i + 1), :], in_=results[i][:])
+
+        permute_wi(0)
+        permute_wi(1)
+        flip_inputs(0)
+        flip_inputs(1)
+        quantise_inputs(0)
+        quantise_inputs(1)
+        flip_inputs(2)
+        flip_inputs(3)
+        quantise_inputs(2)
+        quantise_inputs(3)
         for k in range(AHEAD):
-            drives[k] = first_layer(0, k)
-        spread_bo()
+            first_layer(k)
 
         for k in range(STEPS):
+            q, j = divmod(k, CHAN_TILES)
             if k + AHEAD < SCANS:
-                b, j = divmod(k + AHEAD, CHAN_TILES)
-                drives[k + AHEAD] = first_layer(b, j)
+                first_layer(k + AHEAD)
             if k < SCANS:
-                b, j = divmod(k, CHAN_TILES)
-                recurrence(drives[k], x_lanes[b], j)
-            if 0 <= k - IN_LAG < (BATCH - 1) * PAIRS:
-                quantise_inputs(PAIRS + k - IN_LAG)
-            if 0 <= k - OUT_LAG:
-                b, i = divmod(k - OUT_LAG, TOK_TILES)
-                second_layer(b, s_codes[b], s_scales[b], i)
-            n, chunk = divmod(k - (TILES_PER_PASS - 1) - PACK_LAG, TILES_PER_PASS)
-            if 0 <= n < BATCH * PASSES and chunk < CHUNKS:
-                b, g = divmod(n, PASSES)
-                quantise_x(x_lanes[b], s_codes[b], s_scales[b], g, chunk)
+                recurrence(k)
+            for lag in range(HALVES):
+                done, rest = divmod(k - (PACK - 1) - 1 - lag, PACK)
+                if rest == 0 and 0 <= done < CHUNKS * PASSES:
+                    interleave_x(done // PASSES, done % PASSES, lag)
+                done, rest = divmod(k - (PACK - 1) - 2 - lag, PACK)
+                if rest == 0 and 0 <= done < CHUNKS * PASSES:
+                    quantise_x(done // PASSES, done % PASSES, lag)
+            if q + 1 < CHUNKS and 2 <= j < 2 + UNITS:
+                quantise_inputs(UNITS * (q + 1) + j - 2)
+            if q + 1 < CHUNKS and 1 <= j < 1 + UNITS:
+                flip_inputs(UNITS * (q + 1) + j - 1)
+            if 0 <= k - MM2_LAG < CHUNKS * OUT_UNITS:
+                second_matmul(k - MM2_LAG)
+            if 0 <= k - ADD_LAG:
+                add_bias(k - ADD_LAG)

@@ -21,19 +21,18 @@ PASSES = FEAT // K_PASS
 WIDE = 512
 CHAN_TILES = CHAN // P
 PAIR = 2 * P
+PIECE = PAIR
 CHUNK = WIDE
 CHUNKS = BATCH * SEQ // CHUNK
-CHUNKS_PER_SEQ = SEQ // CHUNK
 UNITS = CHUNK // PAIR * PASSES
-HALVES = 2
-HALF = CHUNK // HALVES
-OUT_UNITS = (CHUNK // P) * (FEAT // WIDE)
-
-SCANS = CHUNKS * CHAN_TILES
+PIECES = CHUNK // PIECE
 AHEAD = 2
-MM2_LAG = 9
-ADD_LAG = 10
-STEPS = SCANS + ADD_LAG
+FLIP_AHEAD = 8
+QIN_LAG = 2
+QX_LAG = 2
+IL_STEP = (0, 1)
+VECTOR_ADDS = (0, 1, 2, 3)
+GPSIMD_PIECES = ()
 
 FLOPS = 2 * BATCH * SEQ * (FEAT * CHAN + CHAN * FEAT)
 
@@ -46,6 +45,7 @@ def tile_slru_kernel(
         ctx.enter_context(tc.manual_schedule())
         keep = ctx.enter_context(tc.tile_pool(name="keep", bufs=1))
         stream = ctx.enter_context(tc.tile_pool(name="stream", bufs=4))
+        wide = ctx.enter_context(tc.tile_pool(name="wide", bufs=2))
         flip_psum = ctx.enter_context(tc.psum_pool(name="flip_psum", bufs=2))
         first_psum = ctx.enter_context(tc.psum_pool(name="first_psum", bufs=3))
         second_psum = ctx.enter_context(tc.psum_pool(name="second_psum", bufs=3))
@@ -83,30 +83,43 @@ def tile_slru_kernel(
         x_rows = keep.tile([P, BATCH * SEQ // P, FEAT], BF16)
         x_dram = inputs.rearrange("b (i p) f -> p (b i) f", p=P)
 
-        def load_tokens(pair):
-            tiles = slice(2 * pair, 2 * pair + 2)
+        def load_tokens(first_tile, n_tiles):
+            tiles = slice(first_tile, first_tile + n_tiles)
             nc.sync.dma_start(out=x_rows[:, tiles, :], in_=x_dram[:, tiles, :])
 
-        wi_raw = keep.tile([P, PASSES, CHAN], U32, align_bytes=64)
-        wi_codes = keep.tile([P, PASSES, CHAN], U32, align_bytes=64)
-        wi_sc = keep.tile([P, CHAN], U8, align_bytes=64)
-        wo_codes = keep.tile([P, PASSES, FEAT], U32, align_bytes=64)
+        wi_raw = [
+            keep.tile([P, PASSES, K_PASS], U32, align_bytes=64, name="wi_raw%d" % grp)
+            for grp in range(PASSES)
+        ]
+        wi_codes = [
+            keep.tile([P, PASSES, K_PASS], U32, align_bytes=64, name="wi_codes%d" % grp)
+            for grp in range(PASSES)
+        ]
+        wi_sc = [
+            keep.tile([P, K_PASS], U8, align_bytes=64, name="wi_sc%d" % grp) for grp in range(PASSES)
+        ]
+        wo_codes = [
+            keep.tile([P, PASSES, WIDE], U32, align_bytes=64, name="wo_codes%d" % half)
+            for half in range(FEAT // WIDE)
+        ]
 
-        def load_weight_codes(codes, words, first_col, n_cols):
-            cols = slice(first_col, first_col + n_cols)
+        def load_weight_codes(codes, words, part):
+            cols = slice(K_PASS * part, K_PASS * (part + 1))
             nc.sync.dma_start(
-                out=codes[:, :, cols].bitcast(I32),
+                out=codes[part][:].bitcast(I32),
                 in_=words.rearrange("g p n t -> p g (n t)").bitcast(I32)[:, :, cols],
             )
 
         load_weight_scales(wi_sc_raw, Wi_scales)
+        load_weight_codes(wi_raw, Wi_words, 0)
+        load_tokens(0, 2)
+        load_tokens(2, 2)
+        load_weight_codes(wi_raw, Wi_words, 1)
+        for pair in range(2, BATCH * SEQ // PAIR):
+            load_tokens(2 * pair, 2)
         load_weight_scales(wo_sc, Wo_scales)
-        load_weight_codes(wi_raw, Wi_words, 0, K_PASS)
-        load_weight_codes(wi_raw, Wi_words, K_PASS, K_PASS)
-        for pair in range(BATCH * SEQ // PAIR):
-            load_tokens(pair)
-        for first_col in range(0, FEAT, WIDE):
-            load_weight_codes(wo_codes, Wo_words, first_col, WIDE)
+        for half in range(FEAT // WIDE):
+            load_weight_codes(wo_codes, Wo_words, half)
         bo_all = keep.tile([P, FEAT], BF16)
         nc.sync.dma_start(out=bo_all[:], in_=bo.partition_broadcast(P))
 
@@ -133,62 +146,75 @@ def tile_slru_kernel(
             op=ALU.mult,
         )
 
-        def permute_wi(grp):
+        def permute_scales(grp):
             cols = slice(K_PASS * grp, K_PASS * (grp + 1))
             nc.vector.tensor_copy(
-                out=wi_sc[:, cols].rearrange("p (t m) -> p m t", t=PACK),
+                out=wi_sc[grp][:].rearrange("p (t m) -> p m t", t=PACK),
                 in_=wi_sc_raw[:, cols].rearrange("p (m t) -> p m t", t=PACK),
             )
+
+        def permute_codes(grp):
             nc.vector.tensor_copy(
-                out=wi_codes[:].bitcast(I32)[:, :, cols].rearrange("p g (t m) -> p g t m", t=PACK),
-                in_=wi_raw[:].bitcast(I32)[:, :, cols].rearrange("p g (m t) -> p g t m", t=PACK),
+                out=wi_codes[grp][:].bitcast(I32).rearrange("p g (t m) -> p g t m", t=PACK),
+                in_=wi_raw[grp][:].bitcast(I32).rearrange("p g (m t) -> p g t m", t=PACK),
             )
 
-        x_codes = keep.tile([P, PASSES, BATCH * SEQ], U32, align_bytes=64)
-        x_scales = keep.tile([P, PASSES, BATCH * SEQ], U8, align_bytes=64)
+        x_codes = keep.tile([P, CHUNKS, PASSES, CHUNK], U32, align_bytes=64)
+        x_scales = keep.tile([P, CHUNKS, PASSES, CHUNK], U8, align_bytes=64)
         grouped_in = {}
 
         def flip_inputs(unit):
-            pair, g = divmod(unit, PASSES)
+            c, rest = divmod(unit, UNITS)
+            h, g = divmod(rest, PASSES)
+            if rest == 0:
+                grouped_in[c] = wide.tile(
+                    [P, PASSES, CHUNK * PACK], BF16, align_bytes=64, name="gin%d" % c, tag="grouped_in"
+                )
             flipped = flip_psum.tile([P, 2, PAIR], F32, tag="flip")
             for i in range(2):
-                words = x_rows[:, 2 * pair + i, :].bitcast(F32)
+                words = x_rows[:, (CHUNK // P) * c + 2 * h + i, :].bitcast(F32)
                 for u in range(2):
                     nc.tensor.transpose(
                         flipped[:, u, P * i : P * (i + 1)],
                         words[:, 2 * P * g + u : 2 * P * (g + 1) : 2],
                         ident_f32[:],
                     )
-            grouped = stream.tile([P, PAIR * PACK], BF16, align_bytes=64, tag="grouped_in")
             nc.scalar.copy(
-                out=grouped[:].bitcast(F32).rearrange("p (r u) -> p r u", u=2),
+                out=grouped_in[c][:, g, PAIR * PACK * h : PAIR * PACK * (h + 1)]
+                .bitcast(F32)
+                .rearrange("p (r u) -> p r u", u=2),
                 in_=flipped[:].rearrange("p u r -> p r u"),
             )
-            grouped_in[unit] = grouped
 
-        def quantise_inputs(unit):
-            pair, g = divmod(unit, PASSES)
-            tokens = slice(PAIR * pair, PAIR * (pair + 1))
+        def quantise_unit(unit):
+            c, rest = divmod(unit, UNITS)
+            h, g = divmod(rest, PASSES)
             nc.vector.quantize_mx(
-                out=x_codes[:, g, tokens].bitcast(FP8X4),
-                scales=x_scales[:, g, tokens],
-                in_=grouped_in[unit][:],
+                out=x_codes[:, c, g, PAIR * h : PAIR * (h + 1)].bitcast(FP8X4),
+                scales=x_scales[:, c, g, PAIR * h : PAIR * (h + 1)],
+                in_=grouped_in[c][:, g, PAIR * PACK * h : PAIR * PACK * (h + 1)],
+            )
+
+        def quantise_chunk(c):
+            nc.vector.quantize_mx(
+                out=x_codes[:, c, :, :].rearrange("p g n -> p (g n)").bitcast(FP8X4),
+                scales=x_scales[:, c, :, :].rearrange("p g n -> p (g n)"),
+                in_=grouped_in[c][:].rearrange("p g n -> p (g n)"),
             )
 
         drives = {}
 
-        def first_layer(k):
-            q, j = divmod(k, CHAN_TILES)
-            chans = slice(P * j, P * (j + 1))
-            tokens = slice(q * CHUNK, (q + 1) * CHUNK)
-            acc = first_psum.tile([P, WIDE], F32, tag="first")
+        def first_layer(c, j):
+            grp, t = divmod(j, PACK)
+            chans = slice(P * t, P * (t + 1))
+            acc = first_psum.tile([P, CHUNK], F32, tag="first")
             for g in range(PASSES):
                 nc.tensor.matmul_mx(
                     out=acc[:],
-                    lhsT=wi_codes[:, g, chans].bitcast(FP8X4),
-                    lhsT_scale=wi_sc[plane(g) : P, chans],
-                    rhs=x_codes[:, g, tokens].bitcast(FP8X4),
-                    rhs_scale=x_scales[:, g, tokens],
+                    lhsT=wi_codes[grp][:, g, chans].bitcast(FP8X4),
+                    lhsT_scale=wi_sc[grp][plane(g) : P, chans],
+                    rhs=x_codes[:, c, g, :].bitcast(FP8X4),
+                    rhs_scale=x_scales[:, c, g, :],
                     start=(g == 0),
                     stop=(g == PASSES - 1),
                 )
@@ -200,25 +226,24 @@ def tile_slru_kernel(
                 scale=gamma[:, j : j + 1],
                 bias=gamma_bi[:, j : j + 1],
             )
-            drives[k] = drive
+            drives[(c, j)] = drive
 
         states = {}
 
-        def recurrence(k):
-            q, j = divmod(k, CHAN_TILES)
+        def recurrence(c, j):
             grp, t = divmod(j, PACK)
             if t == 0:
-                states[(q, grp)] = stream.tile(
-                    [P, PACK, CHUNK], F32, name="state%d_%d" % (q, grp), tag="state"
+                states[(c, grp)] = stream.tile(
+                    [P, PACK, CHUNK], F32, name="state%d_%d" % (c, grp), tag="state"
                 )
-            if q % CHUNKS_PER_SEQ == 0:
+            if c * CHUNK % SEQ == 0:
                 carry = 0.0
             else:
-                carry = states[(q - 1, grp)][:, t, CHUNK - 1 : CHUNK]
+                carry = states[(c - 1, grp)][:, t, CHUNK - 1 : CHUNK]
             nc.vector.tensor_tensor_scan(
-                out=states[(q, grp)][:, t, :],
+                out=states[(c, grp)][:, t, :],
                 data0=decay[:, j : j + 1].to_broadcast([P, CHUNK]),
-                data1=drives[k][:],
+                data1=drives[(c, j)][:],
                 initial=carry,
                 op0=ALU.mult,
                 op1=ALU.add,
@@ -228,21 +253,28 @@ def tile_slru_kernel(
         s_scales = keep.tile([P, PASSES, BATCH * SEQ], U8, align_bytes=64)
         grouped_x = {}
 
-        def interleave_x(q, grp, piece):
-            local = slice(piece * HALF, (piece + 1) * HALF)
-            grouped = stream.tile([P, HALF, PACK], BF16, align_bytes=64, tag="grouped_x")
-            nc.scalar.copy(
-                out=grouped[:].rearrange("p (c i) t -> p c t i", i=4),
-                in_=states[(q, grp)][:, :, local].rearrange("p t (c i) -> p c t i", i=4),
-            )
-            grouped_x[(q, grp, piece)] = grouped
+        def interleave_x(c, grp, piece):
+            local = slice(piece * PIECE, (piece + 1) * PIECE)
+            if piece == 0:
+                grouped_x[(c, grp)] = stream.tile(
+                    [P, CHUNK, PACK], BF16, align_bytes=64, name="gx%d_%d" % (c, grp), tag="grouped_x"
+                )
+            dst = grouped_x[(c, grp)][:, local, :].rearrange("p (c i) t -> p c t i", i=4)
+            src = states[(c, grp)][:, :, local].rearrange("p t (c i) -> p c t i", i=4)
+            if piece in GPSIMD_PIECES:
+                nc.gpsimd.tensor_scalar(
+                    out=dst, in0=src, scalar1=1.0, scalar2=0.0, op0=ALU.mult, op1=ALU.add
+                )
+            else:
+                nc.scalar.copy(out=dst, in_=src)
 
-        def quantise_x(q, grp, piece):
-            tokens = slice(q * CHUNK + piece * HALF, q * CHUNK + (piece + 1) * HALF)
+        def quantise_x(c, grp, first_piece, n_pieces):
+            local = slice(first_piece * PIECE, (first_piece + n_pieces) * PIECE)
+            tokens = slice(c * CHUNK + local.start, c * CHUNK + local.stop)
             nc.vector.quantize_mx(
                 out=s_codes[:, grp, tokens].bitcast(FP8X4),
                 scales=s_scales[:, grp, tokens],
-                in_=grouped_x[(q, grp, piece)][:].rearrange("p r t -> p (r t)"),
+                in_=grouped_x[(c, grp)][:, local, :].rearrange("p r t -> p (r t)"),
             )
 
         sums = {}
@@ -258,7 +290,7 @@ def tile_slru_kernel(
                     out=acc[:],
                     lhsT=s_codes[:, g, toks].bitcast(FP8X4),
                     lhsT_scale=s_scales[:, g, toks],
-                    rhs=wo_codes[:, g, cols].bitcast(FP8X4),
+                    rhs=wo_codes[half][:, g, :].bitcast(FP8X4),
                     rhs_scale=wo_sc[plane(g) : P, cols],
                     start=(g == 0),
                     stop=(g == PASSES - 1),
@@ -272,43 +304,73 @@ def tile_slru_kernel(
             cols = slice(WIDE * half, WIDE * (half + 1))
             if half == 0:
                 results[i] = stream.tile([P, FEAT], F32, name="result%d" % i, tag="result")
-            nc.vector.tensor_tensor(
-                out=results[i][:, cols], in0=sums[n][:], in1=bo_all[:, cols], op=ALU.add
-            )
+            if n % 4 in VECTOR_ADDS:
+                nc.vector.tensor_tensor(
+                    out=results[i][:, cols], in0=sums[n][:], in1=bo_all[:, cols], op=ALU.add
+                )
+            else:
+                nc.scalar.copy(out=results[i][:, cols], in_=sums[n][:])
+                nc.gpsimd.tensor_tensor(
+                    out=results[i][:, cols], in0=results[i][:, cols], in1=bo_all[:, cols], op=ALU.add
+                )
             if half == FEAT // WIDE - 1:
                 nc.sync.dma_start(out=out_rows[P * i : P * (i + 1), :], in_=results[i][:])
 
-        permute_wi(0)
-        permute_wi(1)
-        flip_inputs(0)
-        flip_inputs(1)
-        quantise_inputs(0)
-        quantise_inputs(1)
-        flip_inputs(2)
-        flip_inputs(3)
-        quantise_inputs(2)
-        quantise_inputs(3)
-        for k in range(AHEAD):
-            first_layer(k)
+        scans = [(c, j) for c in range(CHUNKS) for j in range(CHAN_TILES)]
+        flip_at = {}
+        quantise_in_at = {}
+        interleave_at = {}
+        quantise_x_at = {}
+        for c in range(1, CHUNKS):
+            for a in range(UNITS):
+                flip_at[CHAN_TILES * c - FLIP_AHEAD + a] = UNITS * c + a
+            quantise_in_at[CHAN_TILES * c - FLIP_AHEAD + UNITS - 1 + QIN_LAG] = c
+        for c in range(CHUNKS):
+            for grp in range(PASSES):
+                done = CHAN_TILES * c + PACK * (grp + 1)
+                last = (c, grp) == (CHUNKS - 1, PASSES - 1)
+                for piece in range(PIECES):
+                    at = done + IL_STEP[piece]
+                    interleave_at.setdefault(at, []).append((c, grp, piece))
+                    if last:
+                        quantise_x_at.setdefault(at + 1, []).append((c, grp, piece, 1))
+                if not last:
+                    quantise_x_at.setdefault(done + max(IL_STEP) + QX_LAG, []).append((c, grp, 0, PIECES))
 
-        for k in range(STEPS):
-            q, j = divmod(k, CHAN_TILES)
-            if k + AHEAD < SCANS:
-                first_layer(k + AHEAD)
-            if k < SCANS:
-                recurrence(k)
-            for lag in range(HALVES):
-                done, rest = divmod(k - (PACK - 1) - 1 - lag, PACK)
-                if rest == 0 and 0 <= done < CHUNKS * PASSES:
-                    interleave_x(done // PASSES, done % PASSES, lag)
-                done, rest = divmod(k - (PACK - 1) - 2 - lag, PACK)
-                if rest == 0 and 0 <= done < CHUNKS * PASSES:
-                    quantise_x(done // PASSES, done % PASSES, lag)
-            if q + 1 < CHUNKS and 2 <= j < 2 + UNITS:
-                quantise_inputs(UNITS * (q + 1) + j - 2)
-            if q + 1 < CHUNKS and 1 <= j < 1 + UNITS:
-                flip_inputs(UNITS * (q + 1) + j - 1)
-            if 0 <= k - MM2_LAG < CHUNKS * OUT_UNITS:
-                second_matmul(k - MM2_LAG)
-            if 0 <= k - ADD_LAG:
-                add_bias(k - ADD_LAG)
+        permute_scales(0)
+        permute_scales(1)
+        permute_codes(0)
+        for unit in range(UNITS):
+            flip_inputs(unit)
+            quantise_unit(unit)
+        permute_codes(1)
+        for k in range(AHEAD):
+            first_layer(scans[k][0], scans[k][1])
+
+        n_units = BATCH * SEQ // P * (FEAT // WIDE)
+        per_piece = PIECE // P * (FEAT // WIDE)
+        ready = 0
+        multiplied = 0
+        added = 0
+        for k in range(len(scans) + n_units):
+            if k + AHEAD < len(scans):
+                first_layer(scans[k + AHEAD][0], scans[k + AHEAD][1])
+            if k < len(scans):
+                recurrence(scans[k][0], scans[k][1])
+            for c, grp, piece, n_pieces in quantise_x_at.get(k, []):
+                quantise_x(c, grp, piece, n_pieces)
+                if grp == PASSES - 1:
+                    ready += n_pieces * per_piece
+            for c, grp, piece in interleave_at.get(k, []):
+                interleave_x(c, grp, piece)
+            if k in quantise_in_at:
+                quantise_chunk(quantise_in_at[k])
+            if k in flip_at:
+                flip_inputs(flip_at[k])
+            if added < multiplied:
+                add_bias(added)
+                added += 1
+            if multiplied < ready:
+                second_matmul(multiplied)
+                multiplied += 1
+        assert added == n_units

@@ -31,8 +31,8 @@ FLIP_AHEAD = 8
 QIN_LAG = 2
 QX_LAG = 2
 IL_STEP = (0, 1)
-VECTOR_ADDS = (0, 1, 2, 3)
-GPSIMD_PIECES = ()
+VECTOR_ADDS = (0, 2)
+GPSIMD_PIECES = (1,)
 
 FLOPS = 2 * BATCH * SEQ * (FEAT * CHAN + CHAN * FEAT)
 
@@ -47,7 +47,8 @@ def tile_slru_kernel(
         stream = ctx.enter_context(tc.tile_pool(name="stream", bufs=4))
         wide = ctx.enter_context(tc.tile_pool(name="wide", bufs=2))
         flip_psum = ctx.enter_context(tc.psum_pool(name="flip_psum", bufs=2))
-        first_psum = ctx.enter_context(tc.psum_pool(name="first_psum", bufs=3))
+        first_psum = ctx.enter_context(tc.psum_pool(name="first_psum", bufs=2))
+        const_psum = ctx.enter_context(tc.psum_pool(name="const_psum", bufs=1))
         second_psum = ctx.enter_context(tc.psum_pool(name="second_psum", bufs=3))
 
         par = keep.tile([P, 3 * PASSES, PACK], BF16)
@@ -132,6 +133,8 @@ def tile_slru_kernel(
         )
         decay = keep.tile([P, CHAN_TILES], F32)
         nc.scalar.activation(out=decay[:], in_=nu[:], func=ACT.Exp, scale=-1.0)
+        decay_psum = const_psum.tile([P, CHAN_TILES], F32)
+        nc.tensor.matmul(out=decay_psum[:], lhsT=ident_f32[:], rhs=decay[:], start=True, stop=True)
         gamma = keep.tile([P, CHAN_TILES], F32)
         nc.scalar.activation(
             out=gamma[:],
@@ -242,7 +245,7 @@ def tile_slru_kernel(
                 carry = states[(c - 1, grp)][:, t, CHUNK - 1 : CHUNK]
             nc.vector.tensor_tensor_scan(
                 out=states[(c, grp)][:, t, :],
-                data0=decay[:, j : j + 1].to_broadcast([P, CHUNK]),
+                data0=decay_psum[:, j : j + 1].to_broadcast([P, CHUNK]),
                 data1=drives[(c, j)][:],
                 initial=carry,
                 op0=ALU.mult,

@@ -21,16 +21,15 @@ PASSES = FEAT // K_PASS
 WIDE = 512
 CHAN_TILES = CHAN // P
 PAIR = 2 * P
-PIECE = PAIR
-CHUNK = WIDE
-CHUNKS = BATCH * SEQ // CHUNK
-UNITS = CHUNK // PAIR * PASSES
-PIECES = CHUNK // PIECE
+TOKENS = BATCH * SEQ
+CHUNK_LENS = (WIDE, WIDE, WIDE, PAIR, PAIR)
+assert sum(CHUNK_LENS) == TOKENS
 AHEAD = 2
 FLIP_AHEAD = 8
 QIN_LAG = 2
-QX_LAG = 2
-IL_STEP = (0, 1)
+QX_LAG = 3
+VECTOR_TAIL = 8
+TAIL_UNITS = CHUNK_LENS[-1] // P * (FEAT // WIDE)
 VECTOR_ADDS = (0, 2)
 GPSIMD_PIECES = (1,)
 
@@ -81,7 +80,7 @@ def tile_slru_kernel(
                     in_=scales.bitcast(I32)[:, 4 * quad : 4 * quad + 4, :],
                 )
 
-        x_rows = keep.tile([P, BATCH * SEQ // P, FEAT], BF16)
+        x_rows = keep.tile([P, TOKENS // P, FEAT], BF16)
         x_dram = inputs.rearrange("b (i p) f -> p (b i) f", p=P)
 
         def load_tokens(first_tile, n_tiles):
@@ -116,7 +115,7 @@ def tile_slru_kernel(
         load_tokens(0, 2)
         load_tokens(2, 2)
         load_weight_codes(wi_raw, Wi_words, 1)
-        for pair in range(2, BATCH * SEQ // PAIR):
+        for pair in range(2, TOKENS // PAIR):
             load_tokens(2 * pair, 2)
         load_weight_scales(wo_sc, Wo_scales)
         for half in range(FEAT // WIDE):
@@ -162,20 +161,32 @@ def tile_slru_kernel(
                 in_=wi_raw[grp][:].bitcast(I32).rearrange("p g (m t) -> p g t m", t=PACK),
             )
 
-        x_codes = keep.tile([P, CHUNKS, PASSES, CHUNK], U32, align_bytes=64)
-        x_scales = keep.tile([P, CHUNKS, PASSES, CHUNK], U8, align_bytes=64)
+        chunks = []
+        for n_tokens in CHUNK_LENS:
+            chunks.append((sum(CHUNK_LENS[: len(chunks)]), n_tokens))
+        chunk_of_pair = {}
+        for c in range(len(chunks)):
+            for h in range(chunks[c][1] // PAIR):
+                chunk_of_pair[chunks[c][0] // PAIR + h] = (c, h)
+
+        x_codes = keep.tile([P, PASSES * TOKENS], U32, align_bytes=64)
+        x_scales = keep.tile([P, PASSES * TOKENS], U8, align_bytes=64)
         grouped_in = {}
 
+        def x_cols(c, g, first, n_cols):
+            start = PASSES * chunks[c][0] + g * chunks[c][1] + first
+            return slice(start, start + n_cols)
+
         def flip_inputs(unit):
-            c, rest = divmod(unit, UNITS)
-            h, g = divmod(rest, PASSES)
-            if rest == 0:
+            pair, g = divmod(unit, PASSES)
+            c, h = chunk_of_pair[pair]
+            if (h, g) == (0, 0):
                 grouped_in[c] = wide.tile(
-                    [P, PASSES, CHUNK * PACK], BF16, align_bytes=64, name="gin%d" % c, tag="grouped_in"
+                    [P, PASSES, chunks[c][1] * PACK], BF16, align_bytes=64, name="gin%d" % c, tag="grouped_in"
                 )
             flipped = flip_psum.tile([P, 2, PAIR], F32, tag="flip")
             for i in range(2):
-                words = x_rows[:, (CHUNK // P) * c + 2 * h + i, :].bitcast(F32)
+                words = x_rows[:, 2 * pair + i, :].bitcast(F32)
                 for u in range(2):
                     nc.tensor.transpose(
                         flipped[:, u, P * i : P * (i + 1)],
@@ -190,18 +201,19 @@ def tile_slru_kernel(
             )
 
         def quantise_unit(unit):
-            c, rest = divmod(unit, UNITS)
-            h, g = divmod(rest, PASSES)
+            pair, g = divmod(unit, PASSES)
+            c, h = chunk_of_pair[pair]
             nc.vector.quantize_mx(
-                out=x_codes[:, c, g, PAIR * h : PAIR * (h + 1)].bitcast(FP8X4),
-                scales=x_scales[:, c, g, PAIR * h : PAIR * (h + 1)],
+                out=x_codes[:, x_cols(c, g, PAIR * h, PAIR)].bitcast(FP8X4),
+                scales=x_scales[:, x_cols(c, g, PAIR * h, PAIR)],
                 in_=grouped_in[c][:, g, PAIR * PACK * h : PAIR * PACK * (h + 1)],
             )
 
         def quantise_chunk(c):
+            cols = x_cols(c, 0, 0, PASSES * chunks[c][1])
             nc.vector.quantize_mx(
-                out=x_codes[:, c, :, :].rearrange("p g n -> p (g n)").bitcast(FP8X4),
-                scales=x_scales[:, c, :, :].rearrange("p g n -> p (g n)"),
+                out=x_codes[:, cols].bitcast(FP8X4),
+                scales=x_scales[:, cols],
                 in_=grouped_in[c][:].rearrange("p g n -> p (g n)"),
             )
 
@@ -210,21 +222,22 @@ def tile_slru_kernel(
         def first_layer(c, j):
             grp, t = divmod(j, PACK)
             chans = slice(P * t, P * (t + 1))
-            acc = first_psum.tile([P, CHUNK], F32, tag="first")
+            n_tokens = chunks[c][1]
+            acc = first_psum.tile([P, WIDE], F32, tag="first")
             for g in range(PASSES):
                 nc.tensor.matmul_mx(
-                    out=acc[:],
+                    out=acc[:, 0:n_tokens],
                     lhsT=wi_codes[grp][:, g, chans].bitcast(FP8X4),
                     lhsT_scale=wi_sc[grp][plane(g) : P, chans],
-                    rhs=x_codes[:, c, g, :].bitcast(FP8X4),
-                    rhs_scale=x_scales[:, c, g, :],
+                    rhs=x_codes[:, x_cols(c, g, 0, n_tokens)].bitcast(FP8X4),
+                    rhs_scale=x_scales[:, x_cols(c, g, 0, n_tokens)],
                     start=(g == 0),
                     stop=(g == PASSES - 1),
                 )
-            drive = stream.tile([P, CHUNK], F32, tag="drive")
+            drive = stream.tile([P, WIDE], F32, tag="drive")
             nc.scalar.activation(
-                out=drive[:],
-                in_=acc[:],
+                out=drive[:, 0:n_tokens],
+                in_=acc[:, 0:n_tokens],
                 func=ACT.Identity,
                 scale=gamma[:, j : j + 1],
                 bias=gamma_bi[:, j : j + 1],
@@ -234,71 +247,86 @@ def tile_slru_kernel(
         states = {}
 
         def recurrence(c, j):
+            first, n_tokens = chunks[c]
             grp, t = divmod(j, PACK)
             if t == 0:
                 states[(c, grp)] = stream.tile(
-                    [P, PACK, CHUNK], F32, name="state%d_%d" % (c, grp), tag="state"
+                    [P, PACK, WIDE], F32, name="state%d_%d" % (c, grp), tag="state"
                 )
-            if c * CHUNK % SEQ == 0:
+            if first % SEQ == 0:
                 carry = 0.0
             else:
-                carry = states[(c - 1, grp)][:, t, CHUNK - 1 : CHUNK]
+                last = chunks[c - 1][1] - 1
+                carry = states[(c - 1, grp)][:, t, last : last + 1]
             nc.vector.tensor_tensor_scan(
-                out=states[(c, grp)][:, t, :],
-                data0=decay_psum[:, j : j + 1].to_broadcast([P, CHUNK]),
-                data1=drives[(c, j)][:],
+                out=states[(c, grp)][:, t, 0:n_tokens],
+                data0=decay_psum[:, j : j + 1].to_broadcast([P, n_tokens]),
+                data1=drives[(c, j)][:, 0:n_tokens],
                 initial=carry,
                 op0=ALU.mult,
                 op1=ALU.add,
             )
 
-        s_codes = keep.tile([P, PASSES, BATCH * SEQ], U32, align_bytes=64)
-        s_scales = keep.tile([P, PASSES, BATCH * SEQ], U8, align_bytes=64)
+        s_codes = keep.tile([P, PASSES, TOKENS], U32, align_bytes=64)
+        s_scales = keep.tile([P, PASSES, TOKENS], U8, align_bytes=64)
         grouped_x = {}
 
         def interleave_x(c, grp, piece):
-            local = slice(piece * PIECE, (piece + 1) * PIECE)
+            n_tokens = chunks[c][1]
+            local = slice(piece * n_tokens // 2, (piece + 1) * n_tokens // 2)
             if piece == 0:
                 grouped_x[(c, grp)] = stream.tile(
-                    [P, CHUNK, PACK], BF16, align_bytes=64, name="gx%d_%d" % (c, grp), tag="grouped_x"
+                    [P, n_tokens, PACK], BF16, align_bytes=64, name="gx%d_%d" % (c, grp), tag="grouped_x"
                 )
             dst = grouped_x[(c, grp)][:, local, :].rearrange("p (c i) t -> p c t i", i=4)
             src = states[(c, grp)][:, :, local].rearrange("p t (c i) -> p c t i", i=4)
-            if piece in GPSIMD_PIECES:
+            if (c, grp, piece) == (len(chunks) - 1, PASSES - 1, 1):
+                nc.vector.tensor_copy(out=dst, in_=src)
+            elif piece in GPSIMD_PIECES and n_tokens == WIDE:
                 nc.gpsimd.tensor_scalar(
                     out=dst, in0=src, scalar1=1.0, scalar2=0.0, op0=ALU.mult, op1=ALU.add
                 )
             else:
                 nc.scalar.copy(out=dst, in_=src)
 
-        def quantise_x(c, grp, first_piece, n_pieces):
-            local = slice(first_piece * PIECE, (first_piece + n_pieces) * PIECE)
-            tokens = slice(c * CHUNK + local.start, c * CHUNK + local.stop)
+        def quantise_x(c, grp):
+            first, n_tokens = chunks[c]
+            tokens = slice(first, first + n_tokens)
             nc.vector.quantize_mx(
                 out=s_codes[:, grp, tokens].bitcast(FP8X4),
                 scales=s_scales[:, grp, tokens],
-                in_=grouped_x[(c, grp)][:, local, :].rearrange("p r t -> p (r t)"),
+                in_=grouped_x[(c, grp)][:].rearrange("p r t -> p (r t)"),
             )
 
         sums = {}
         results = {}
+        n_units = TOKENS // P * (FEAT // WIDE)
 
-        def second_matmul(n):
+        def second_pass(n, g):
             i, half = divmod(n, FEAT // WIDE)
             toks = slice(P * i, P * (i + 1))
             cols = slice(WIDE * half, WIDE * (half + 1))
-            acc = second_psum.tile([P, WIDE], F32, tag="second")
+            nc.tensor.matmul_mx(
+                out=sums[n][:],
+                lhsT=s_codes[:, g, toks].bitcast(FP8X4),
+                lhsT_scale=s_scales[:, g, toks],
+                rhs=wo_codes[half][:, g, :].bitcast(FP8X4),
+                rhs_scale=wo_sc[plane(g) : P, cols],
+                start=(g == 0),
+                stop=(g == PASSES - 1),
+            )
+
+        def second_matmul(n):
+            sums[n] = second_psum.tile([P, WIDE], F32, name="sum%d" % n, tag="second")
             for g in range(PASSES):
-                nc.tensor.matmul_mx(
-                    out=acc[:],
-                    lhsT=s_codes[:, g, toks].bitcast(FP8X4),
-                    lhsT_scale=s_scales[:, g, toks],
-                    rhs=wo_codes[half][:, g, :].bitcast(FP8X4),
-                    rhs_scale=wo_sc[plane(g) : P, cols],
-                    start=(g == 0),
-                    stop=(g == PASSES - 1),
-                )
-            sums[n] = acc
+                second_pass(n, g)
+
+        def open_tail(n):
+            if n % 2 == 0:
+                sums[n] = first_psum.tile([P, WIDE], F32, name="sum%d" % n, tag="first")
+            else:
+                sums[n] = flip_psum.tile([P, WIDE], F32, name="sum%d" % n, tag="flip")
+            second_pass(n, 0)
 
         out_rows = out.rearrange("b s f -> (b s) f")
 
@@ -307,7 +335,7 @@ def tile_slru_kernel(
             cols = slice(WIDE * half, WIDE * (half + 1))
             if half == 0:
                 results[i] = stream.tile([P, FEAT], F32, name="result%d" % i, tag="result")
-            if n % 4 in VECTOR_ADDS:
+            if n % 4 in VECTOR_ADDS or n >= n_units - VECTOR_TAIL:
                 nc.vector.tensor_tensor(
                     out=results[i][:, cols], in0=sums[n][:], in1=bo_all[:, cols], op=ALU.add
                 )
@@ -316,42 +344,38 @@ def tile_slru_kernel(
                 nc.gpsimd.tensor_tensor(
                     out=results[i][:, cols], in0=results[i][:, cols], in1=bo_all[:, cols], op=ALU.add
                 )
-            if half == FEAT // WIDE - 1:
+            if n >= n_units - TAIL_UNITS:
+                nc.sync.dma_start(out=out_rows[P * i : P * (i + 1), cols], in_=results[i][:, cols])
+            elif half == FEAT // WIDE - 1:
                 nc.sync.dma_start(out=out_rows[P * i : P * (i + 1), :], in_=results[i][:])
 
-        scans = [(c, j) for c in range(CHUNKS) for j in range(CHAN_TILES)]
+        scans = [(c, j) for c in range(len(chunks)) for j in range(CHAN_TILES)]
         flip_at = {}
         quantise_in_at = {}
         interleave_at = {}
         quantise_x_at = {}
-        for c in range(1, CHUNKS):
-            for a in range(UNITS):
-                flip_at[CHAN_TILES * c - FLIP_AHEAD + a] = UNITS * c + a
-            quantise_in_at[CHAN_TILES * c - FLIP_AHEAD + UNITS - 1 + QIN_LAG] = c
-        for c in range(CHUNKS):
+        for c in range(1, len(chunks)):
+            units = chunks[c][1] // PAIR * PASSES
+            for a in range(units):
+                flip_at[CHAN_TILES * c - FLIP_AHEAD + a] = chunks[c][0] // PAIR * PASSES + a
+            quantise_in_at[CHAN_TILES * c - FLIP_AHEAD + units - 1 + QIN_LAG] = c
+        for c in range(len(chunks)):
             for grp in range(PASSES):
                 done = CHAN_TILES * c + PACK * (grp + 1)
-                last = (c, grp) == (CHUNKS - 1, PASSES - 1)
-                for piece in range(PIECES):
-                    at = done + IL_STEP[piece]
-                    interleave_at.setdefault(at, []).append((c, grp, piece))
-                    if last:
-                        quantise_x_at.setdefault(at + 1, []).append((c, grp, piece, 1))
-                if not last:
-                    quantise_x_at.setdefault(done + max(IL_STEP) + QX_LAG, []).append((c, grp, 0, PIECES))
+                last = (c, grp) == (len(chunks) - 1, PASSES - 1)
+                interleave_at[done] = (c, grp)
+                quantise_x_at[done + (1 if last else QX_LAG)] = (c, grp)
 
         permute_scales(0)
         permute_scales(1)
         permute_codes(0)
-        for unit in range(UNITS):
+        for unit in range(chunks[0][1] // PAIR * PASSES):
             flip_inputs(unit)
             quantise_unit(unit)
-        permute_codes(1)
         for k in range(AHEAD):
             first_layer(scans[k][0], scans[k][1])
+        permute_codes(1)
 
-        n_units = BATCH * SEQ // P * (FEAT // WIDE)
-        per_piece = PIECE // P * (FEAT // WIDE)
         ready = 0
         multiplied = 0
         added = 0
@@ -360,12 +384,24 @@ def tile_slru_kernel(
                 first_layer(scans[k + AHEAD][0], scans[k + AHEAD][1])
             if k < len(scans):
                 recurrence(scans[k][0], scans[k][1])
-            for c, grp, piece, n_pieces in quantise_x_at.get(k, []):
-                quantise_x(c, grp, piece, n_pieces)
-                if grp == PASSES - 1:
-                    ready += n_pieces * per_piece
-            for c, grp, piece in interleave_at.get(k, []):
-                interleave_x(c, grp, piece)
+            if k in quantise_x_at:
+                c, grp = quantise_x_at[k]
+                quantise_x(c, grp)
+                if c == len(chunks) - 1:
+                    for n in range(n_units - TAIL_UNITS, n_units):
+                        if grp == 0:
+                            open_tail(n)
+                        else:
+                            second_pass(n, grp)
+                    if grp == PASSES - 1:
+                        assert multiplied == n_units - TAIL_UNITS
+                        multiplied = n_units
+                elif grp == PASSES - 1:
+                    ready += chunks[c][1] // P * (FEAT // WIDE)
+            if k in interleave_at:
+                c, grp = interleave_at[k]
+                interleave_x(c, grp, 0)
+                interleave_x(c, grp, 1)
             if k in quantise_in_at:
                 quantise_chunk(quantise_in_at[k])
             if k in flip_at:

@@ -25,12 +25,12 @@ TOKENS = BATCH * SEQ
 CHUNK_LENS = (WIDE, WIDE, WIDE, PAIR, PAIR)
 assert sum(CHUNK_LENS) == TOKENS
 AHEAD = 2
-FLIP_AHEAD = 8
+FLIP_AHEAD = 10
 QIN_LAG = 2
-QX_LAG = 3
-VECTOR_TAIL = 8
+RESULT_BUFS = 7
+GPSIMD_ADDS = 3
 TAIL_UNITS = CHUNK_LENS[-1] // P * (FEAT // WIDE)
-VECTOR_ADDS = (0, 2)
+VECTOR_OF_FOUR = (1, 2, 3, 4, 4)
 GPSIMD_PIECES = (1,)
 
 FLOPS = 2 * BATCH * SEQ * (FEAT * CHAN + CHAN * FEAT)
@@ -45,6 +45,8 @@ def tile_slru_kernel(
         keep = ctx.enter_context(tc.tile_pool(name="keep", bufs=1))
         stream = ctx.enter_context(tc.tile_pool(name="stream", bufs=4))
         wide = ctx.enter_context(tc.tile_pool(name="wide", bufs=2))
+        single = ctx.enter_context(tc.tile_pool(name="single", bufs=1))
+        rows_pool = ctx.enter_context(tc.tile_pool(name="rows_pool", bufs=RESULT_BUFS))
         flip_psum = ctx.enter_context(tc.psum_pool(name="flip_psum", bufs=2))
         first_psum = ctx.enter_context(tc.psum_pool(name="first_psum", bufs=2))
         const_psum = ctx.enter_context(tc.psum_pool(name="const_psum", bufs=1))
@@ -275,14 +277,14 @@ def tile_slru_kernel(
             n_tokens = chunks[c][1]
             local = slice(piece * n_tokens // 2, (piece + 1) * n_tokens // 2)
             if piece == 0:
-                grouped_x[(c, grp)] = stream.tile(
+                grouped_x[(c, grp)] = single.tile(
                     [P, n_tokens, PACK], BF16, align_bytes=64, name="gx%d_%d" % (c, grp), tag="grouped_x"
                 )
             dst = grouped_x[(c, grp)][:, local, :].rearrange("p (c i) t -> p c t i", i=4)
             src = states[(c, grp)][:, :, local].rearrange("p t (c i) -> p c t i", i=4)
             if (c, grp, piece) == (len(chunks) - 1, PASSES - 1, 1):
                 nc.vector.tensor_copy(out=dst, in_=src)
-            elif piece in GPSIMD_PIECES and n_tokens == WIDE:
+            elif piece in GPSIMD_PIECES:
                 nc.gpsimd.tensor_scalar(
                     out=dst, in0=src, scalar1=1.0, scalar2=0.0, op0=ALU.mult, op1=ALU.add
                 )
@@ -330,23 +332,39 @@ def tile_slru_kernel(
 
         out_rows = out.rearrange("b s f -> (b s) f")
 
-        def add_bias(n):
+        def on_vector(n):
+            return n % 4 < VECTOR_OF_FOUR[chunk_of_pair[n // (PAIR // P * (FEAT // WIDE))][0]]
+
+        def empty_bank(n):
             i, half = divmod(n, FEAT // WIDE)
             cols = slice(WIDE * half, WIDE * (half + 1))
             if half == 0:
-                results[i] = stream.tile([P, FEAT], F32, name="result%d" % i, tag="result")
-            if n % 4 in VECTOR_ADDS or n >= n_units - VECTOR_TAIL:
+                results[i] = rows_pool.tile([P, FEAT], F32, name="result%d" % i, tag="result")
+            if on_vector(n):
                 nc.vector.tensor_tensor(
                     out=results[i][:, cols], in0=sums[n][:], in1=bo_all[:, cols], op=ALU.add
                 )
+                finish(n)
             else:
                 nc.scalar.copy(out=results[i][:, cols], in_=sums[n][:])
-                nc.gpsimd.tensor_tensor(
-                    out=results[i][:, cols], in0=results[i][:, cols], in1=bo_all[:, cols], op=ALU.add
-                )
+
+        def gpsimd_add(n):
+            i, half = divmod(n, FEAT // WIDE)
+            cols = slice(WIDE * half, WIDE * (half + 1))
+            nc.gpsimd.tensor_tensor(
+                out=results[i][:, cols], in0=results[i][:, cols], in1=bo_all[:, cols], op=ALU.add
+            )
+            finish(n)
+
+        finished = set()
+
+        def finish(n):
+            i, half = divmod(n, FEAT // WIDE)
+            cols = slice(WIDE * half, WIDE * (half + 1))
+            finished.add(n)
             if n >= n_units - TAIL_UNITS:
                 nc.sync.dma_start(out=out_rows[P * i : P * (i + 1), cols], in_=results[i][:, cols])
-            elif half == FEAT // WIDE - 1:
+            elif all(m in finished for m in range(i * (FEAT // WIDE), (i + 1) * (FEAT // WIDE))):
                 nc.sync.dma_start(out=out_rows[P * i : P * (i + 1), :], in_=results[i][:])
 
         scans = [(c, j) for c in range(len(chunks)) for j in range(CHAN_TILES)]
@@ -357,14 +375,14 @@ def tile_slru_kernel(
         for c in range(1, len(chunks)):
             units = chunks[c][1] // PAIR * PASSES
             for a in range(units):
-                flip_at[CHAN_TILES * c - FLIP_AHEAD + a] = chunks[c][0] // PAIR * PASSES + a
-            quantise_in_at[CHAN_TILES * c - FLIP_AHEAD + units - 1 + QIN_LAG] = c
-        for c in range(len(chunks)):
-            for grp in range(PASSES):
-                done = CHAN_TILES * c + PACK * (grp + 1)
-                last = (c, grp) == (len(chunks) - 1, PASSES - 1)
-                interleave_at[done] = (c, grp)
-                quantise_x_at[done + (1 if last else QX_LAG)] = (c, grp)
+                flip_at[max(CHAN_TILES * c - FLIP_AHEAD, 0) + a] = chunks[c][0] // PAIR * PASSES + a
+            quantise_in_at[CHAN_TILES * c - (PACK if c > 1 else PACK - 1)] = c
+        windows = [(c, grp) for c in range(len(chunks)) for grp in range(PASSES)]
+        for i in range(len(windows)):
+            c, grp = windows[i]
+            done = CHAN_TILES * c + PACK * (grp + 1)
+            interleave_at[done] = (c, grp)
+            quantise_x_at[done + (1 if i == len(windows) - 1 else PACK)] = (c, grp)
 
         permute_scales(0)
         permute_scales(1)
@@ -379,11 +397,12 @@ def tile_slru_kernel(
         ready = 0
         multiplied = 0
         added = 0
+        waiting = []
         for k in range(len(scans) + n_units):
             if k + AHEAD < len(scans):
                 first_layer(scans[k + AHEAD][0], scans[k + AHEAD][1])
-            if k < len(scans):
-                recurrence(scans[k][0], scans[k][1])
+            if k in quantise_in_at:
+                quantise_chunk(quantise_in_at[k])
             if k in quantise_x_at:
                 c, grp = quantise_x_at[k]
                 quantise_x(c, grp)
@@ -398,18 +417,24 @@ def tile_slru_kernel(
                         multiplied = n_units
                 elif grp == PASSES - 1:
                     ready += chunks[c][1] // P * (FEAT // WIDE)
+            if k < len(scans):
+                recurrence(scans[k][0], scans[k][1])
             if k in interleave_at:
                 c, grp = interleave_at[k]
                 interleave_x(c, grp, 0)
                 interleave_x(c, grp, 1)
-            if k in quantise_in_at:
-                quantise_chunk(quantise_in_at[k])
+                for n in waiting[:GPSIMD_ADDS]:
+                    gpsimd_add(n)
+                    waiting.remove(n)
             if k in flip_at:
                 flip_inputs(flip_at[k])
             if added < multiplied:
-                add_bias(added)
+                empty_bank(added)
+                if not on_vector(added):
+                    waiting.append(added)
                 added += 1
             if multiplied < ready:
                 second_matmul(multiplied)
                 multiplied += 1
+        assert not waiting
         assert added == n_units

@@ -28,7 +28,7 @@ AHEAD = 2
 FLIP_AHEAD = 10
 QIN_LAG = 2
 RESULT_BUFS = 7
-GPSIMD_ADDS = 3
+GPSIMD_ADDS = 2
 TAIL_UNITS = CHUNK_LENS[-1] // P * (FEAT // WIDE)
 VECTOR_OF_FOUR = (1, 2, 3, 4, 4)
 GPSIMD_PIECES = (1,)
@@ -394,13 +394,16 @@ def tile_slru_kernel(
             first_layer(scans[k][0], scans[k][1])
         permute_codes(1)
 
+        issued = AHEAD
         ready = 0
         multiplied = 0
         added = 0
         waiting = []
         for k in range(len(scans) + n_units):
-            if k + AHEAD < len(scans):
-                first_layer(scans[k + AHEAD][0], scans[k + AHEAD][1])
+            want = k + AHEAD + (1 if k in interleave_at else 0)
+            for s in range(issued, min(want, len(scans) - 1) + 1):
+                first_layer(scans[s][0], scans[s][1])
+                issued = s + 1
             if k in quantise_in_at:
                 quantise_chunk(quantise_in_at[k])
             if k in quantise_x_at:

@@ -22,15 +22,14 @@ WIDE = 512
 CHAN_TILES = CHAN // P
 PAIR = 2 * P
 TOKENS = BATCH * SEQ
-CHUNK_LENS = (WIDE, WIDE, WIDE, PAIR, PAIR)
+CHUNK_LENS = (PAIR, PAIR, WIDE, WIDE, PAIR, PAIR)
 assert sum(CHUNK_LENS) == TOKENS
 AHEAD = 2
 FLIP_AHEAD = 10
-QIN_LAG = 2
 RESULT_BUFS = 7
 GPSIMD_ADDS = 2
 TAIL_UNITS = CHUNK_LENS[-1] // P * (FEAT // WIDE)
-VECTOR_OF_FOUR = (1, 2, 3, 4, 4)
+VECTOR_OF_FOUR = (1, 1, 2, 3, 4, 4)
 GPSIMD_PIECES = (1,)
 
 FLOPS = 2 * BATCH * SEQ * (FEAT * CHAN + CHAN * FEAT)
@@ -105,23 +104,23 @@ def tile_slru_kernel(
             for half in range(FEAT // WIDE)
         ]
 
-        def load_weight_codes(codes, words, part):
+        def load_weight_codes(codes, words, part, passes):
             cols = slice(K_PASS * part, K_PASS * (part + 1))
             nc.sync.dma_start(
-                out=codes[part][:].bitcast(I32),
-                in_=words.rearrange("g p n t -> p g (n t)").bitcast(I32)[:, :, cols],
+                out=codes[part][:, passes, :].bitcast(I32),
+                in_=words.rearrange("g p n t -> p g (n t)").bitcast(I32)[:, passes, cols],
             )
 
-        load_weight_scales(wi_sc_raw, Wi_scales)
-        load_weight_codes(wi_raw, Wi_words, 0)
         load_tokens(0, 2)
-        load_tokens(2, 2)
-        load_weight_codes(wi_raw, Wi_words, 1)
-        for pair in range(2, TOKENS // PAIR):
+        load_weight_scales(wi_sc_raw, Wi_scales)
+        for g in range(PASSES):
+            load_weight_codes(wi_raw, Wi_words, 0, slice(g, g + 1))
+        load_weight_codes(wi_raw, Wi_words, 1, slice(0, PASSES))
+        for pair in range(1, TOKENS // PAIR):
             load_tokens(2 * pair, 2)
         load_weight_scales(wo_sc, Wo_scales)
         for half in range(FEAT // WIDE):
-            load_weight_codes(wo_codes, Wo_words, half)
+            load_weight_codes(wo_codes, Wo_words, half, slice(0, PASSES))
         bo_all = keep.tile([P, FEAT], BF16)
         nc.sync.dma_start(out=bo_all[:], in_=bo.partition_broadcast(P))
 
@@ -135,7 +134,6 @@ def tile_slru_kernel(
         decay = keep.tile([P, CHAN_TILES], F32)
         nc.scalar.activation(out=decay[:], in_=nu[:], func=ACT.Exp, scale=-1.0)
         decay_psum = const_psum.tile([P, CHAN_TILES], F32)
-        nc.tensor.matmul(out=decay_psum[:], lhsT=ident_f32[:], rhs=decay[:], start=True, stop=True)
         gamma = keep.tile([P, CHAN_TILES], F32)
         nc.scalar.activation(
             out=gamma[:],
@@ -152,15 +150,14 @@ def tile_slru_kernel(
 
         def permute_scales(grp):
             cols = slice(K_PASS * grp, K_PASS * (grp + 1))
-            nc.vector.tensor_copy(
-                out=wi_sc[grp][:].rearrange("p (t m) -> p m t", t=PACK),
-                in_=wi_sc_raw[:, cols].rearrange("p (m t) -> p m t", t=PACK),
-            )
+            raw = wi_sc_raw[:, cols].rearrange("p (m t) -> p t m", t=PACK)
+            for t in range(PACK):
+                nc.vector.tensor_copy(out=wi_sc[grp][:, P * t : P * (t + 1)], in_=raw[:, t, :])
 
-        def permute_codes(grp):
+        def permute_codes(grp, passes):
             nc.vector.tensor_copy(
-                out=wi_codes[grp][:].bitcast(I32).rearrange("p g (t m) -> p g t m", t=PACK),
-                in_=wi_raw[grp][:].bitcast(I32).rearrange("p g (m t) -> p g t m", t=PACK),
+                out=wi_codes[grp][:, passes, :].bitcast(I32).rearrange("p g (t m) -> p g t m", t=PACK),
+                in_=wi_raw[grp][:, passes, :].bitcast(I32).rearrange("p g (m t) -> p g t m", t=PACK),
             )
 
         chunks = []
@@ -221,14 +218,23 @@ def tile_slru_kernel(
 
         drives = {}
 
-        def first_layer(c, j):
+        def first_layers(c, j):
+            n_tokens = chunks[c][1]
+            sums_in = first_psum.tile([P, WIDE], F32, name="first%d_%d" % (c, j), tag="first")
+            parts = [sums_in[:, n_tokens * i : n_tokens * (i + 1)] for i in range(WIDE // n_tokens)]
+            for i in range(len(parts)):
+                multiply_first(c, j + i, parts[i])
+            for i in range(len(parts)):
+                drive_scan(c, j + i, parts[i])
+            return len(parts)
+
+        def multiply_first(c, j, acc):
             grp, t = divmod(j, PACK)
             chans = slice(P * t, P * (t + 1))
             n_tokens = chunks[c][1]
-            acc = first_psum.tile([P, WIDE], F32, tag="first")
             for g in range(PASSES):
                 nc.tensor.matmul_mx(
-                    out=acc[:, 0:n_tokens],
+                    out=acc,
                     lhsT=wi_codes[grp][:, g, chans].bitcast(FP8X4),
                     lhsT_scale=wi_sc[grp][plane(g) : P, chans],
                     rhs=x_codes[:, x_cols(c, g, 0, n_tokens)].bitcast(FP8X4),
@@ -236,10 +242,13 @@ def tile_slru_kernel(
                     start=(g == 0),
                     stop=(g == PASSES - 1),
                 )
+
+        def drive_scan(c, j, acc):
+            n_tokens = chunks[c][1]
             drive = stream.tile([P, WIDE], F32, tag="drive")
             nc.scalar.activation(
                 out=drive[:, 0:n_tokens],
-                in_=acc[:, 0:n_tokens],
+                in_=acc,
                 func=ACT.Identity,
                 scale=gamma[:, j : j + 1],
                 bias=gamma_bi[:, j : j + 1],
@@ -284,7 +293,7 @@ def tile_slru_kernel(
             src = states[(c, grp)][:, :, local].rearrange("p t (c i) -> p c t i", i=4)
             if (c, grp, piece) == (len(chunks) - 1, PASSES - 1, 1):
                 nc.vector.tensor_copy(out=dst, in_=src)
-            elif piece in GPSIMD_PIECES:
+            elif piece in (GPSIMD_PIECES if c >= 2 else (0, 1)):
                 nc.gpsimd.tensor_scalar(
                     out=dst, in0=src, scalar1=1.0, scalar2=0.0, op0=ALU.mult, op1=ALU.add
                 )
@@ -376,7 +385,7 @@ def tile_slru_kernel(
             units = chunks[c][1] // PAIR * PASSES
             for a in range(units):
                 flip_at[max(CHAN_TILES * c - FLIP_AHEAD, 0) + a] = chunks[c][0] // PAIR * PASSES + a
-            quantise_in_at[CHAN_TILES * c - (PACK if c > 1 else PACK - 1)] = c
+            quantise_in_at[CHAN_TILES * c - PACK] = c
         windows = [(c, grp) for c in range(len(chunks)) for grp in range(PASSES)]
         for i in range(len(windows)):
             c, grp = windows[i]
@@ -384,28 +393,28 @@ def tile_slru_kernel(
             interleave_at[done] = (c, grp)
             quantise_x_at[done + (1 if i == len(windows) - 1 else PACK)] = (c, grp)
 
-        permute_scales(0)
-        permute_scales(1)
-        permute_codes(0)
+        for grp in range(PASSES):
+            permute_scales(grp)
+        for g in range(PASSES):
+            permute_codes(0, slice(g, g + 1))
         for unit in range(chunks[0][1] // PAIR * PASSES):
             flip_inputs(unit)
             quantise_unit(unit)
-        for k in range(AHEAD):
-            first_layer(scans[k][0], scans[k][1])
-        permute_codes(1)
-
-        issued = AHEAD
+        permute_codes(1, slice(0, PASSES))
+        nc.tensor.matmul(out=decay_psum[:], lhsT=ident_f32[:], rhs=decay[:], start=True, stop=True)
+        issued = 0
+        while issued < AHEAD:
+            issued += first_layers(scans[issued][0], scans[issued][1])
         ready = 0
         multiplied = 0
         added = 0
         waiting = []
         for k in range(len(scans) + n_units):
-            want = k + AHEAD + (1 if k in interleave_at else 0)
-            for s in range(issued, min(want, len(scans) - 1) + 1):
-                first_layer(scans[s][0], scans[s][1])
-                issued = s + 1
             if k in quantise_in_at:
                 quantise_chunk(quantise_in_at[k])
+            want = k + AHEAD + (1 if k in interleave_at else 0)
+            while issued <= min(want, len(scans) - 1):
+                issued += first_layers(scans[issued][0], scans[issued][1])
             if k in quantise_x_at:
                 c, grp = quantise_x_at[k]
                 quantise_x(c, grp)

@@ -25,11 +25,12 @@ TOKENS = BATCH * SEQ
 CHUNK_LENS = (PAIR, PAIR, WIDE, WIDE, PAIR, PAIR)
 assert sum(CHUNK_LENS) == TOKENS
 AHEAD = 2
-FLIP_AHEAD = 10
+FLIP_STRIDE = 2
+FLIP_AHEAD = 14
 RESULT_BUFS = 7
 GPSIMD_ADDS = 2
 TAIL_UNITS = CHUNK_LENS[-1] // P * (FEAT // WIDE)
-VECTOR_OF_FOUR = (1, 1, 2, 3, 4, 4)
+VECTOR_OF_FOUR = (0, 0, 2, 3, 4, 4)
 GPSIMD_PIECES = (1,)
 
 FLOPS = 2 * BATCH * SEQ * (FEAT * CHAN + CHAN * FEAT)
@@ -56,7 +57,7 @@ def tile_slru_kernel(
             out=par[:, 0 : 2 * PASSES, :],
             in_=params_log.rearrange("r (g p t) -> p (r g) t", p=P, t=PACK),
         )
-        nc.scalar.dma_start(
+        nc.gpsimd.dma_start(
             out=par[:, 2 * PASSES : 3 * PASSES, :],
             in_=bi.rearrange("(g p t) -> p g t", p=P, t=PACK),
         )
@@ -113,8 +114,7 @@ def tile_slru_kernel(
 
         load_tokens(0, 2)
         load_weight_scales(wi_sc_raw, Wi_scales)
-        for g in range(PASSES):
-            load_weight_codes(wi_raw, Wi_words, 0, slice(g, g + 1))
+        load_weight_codes(wi_raw, Wi_words, 0, slice(0, PASSES))
         load_weight_codes(wi_raw, Wi_words, 1, slice(0, PASSES))
         for pair in range(1, TOKENS // PAIR):
             load_tokens(2 * pair, 2)
@@ -382,9 +382,11 @@ def tile_slru_kernel(
         interleave_at = {}
         quantise_x_at = {}
         for c in range(1, len(chunks)):
-            units = chunks[c][1] // PAIR * PASSES
-            for a in range(units):
-                flip_at[max(CHAN_TILES * c - FLIP_AHEAD, 0) + a] = chunks[c][0] // PAIR * PASSES + a
+            first_step = CHAN_TILES * c - FLIP_AHEAD
+            for a in range(chunks[c][1] // PAIR * PASSES):
+                step = a if first_step < 0 else first_step + FLIP_STRIDE * a
+                assert step not in flip_at
+                flip_at[step] = chunks[c][0] // PAIR * PASSES + a
             quantise_in_at[CHAN_TILES * c - PACK] = c
         windows = [(c, grp) for c in range(len(chunks)) for grp in range(PASSES)]
         for i in range(len(windows)):

@@ -278,18 +278,23 @@ def tile_slru_kernel(
                 op1=ALU.add,
             )
 
-        s_codes = keep.tile([P, PASSES, TOKENS], U32, align_bytes=64)
-        s_scales = keep.tile([P, PASSES, TOKENS], U8, align_bytes=64)
+        s_codes = keep.tile([P, PASSES * TOKENS], U32, align_bytes=64)
+        s_scales = keep.tile([P, PASSES * TOKENS], U8, align_bytes=64)
+
+        def s_cols(c, g, first, n_tokens):
+            start = PASSES * chunks[c][0] + g * chunks[c][1] + first
+            return slice(start, start + n_tokens)
+
         grouped_x = {}
 
         def interleave_x(c, grp, piece):
             n_tokens = chunks[c][1]
             local = slice(piece * n_tokens // 2, (piece + 1) * n_tokens // 2)
-            if piece == 0:
-                grouped_x[(c, grp)] = single.tile(
-                    [P, n_tokens, PACK], BF16, align_bytes=64, name="gx%d_%d" % (c, grp), tag="grouped_x"
+            if (grp, piece) == (0, 0):
+                grouped_x[c] = single.tile(
+                    [P, PASSES, n_tokens, PACK], BF16, align_bytes=64, name="gx%d" % c, tag="grouped_x"
                 )
-            dst = grouped_x[(c, grp)][:, local, :].rearrange("p (c i) t -> p c t i", i=4)
+            dst = grouped_x[c][:, grp, local, :].rearrange("p (c i) t -> p c t i", i=4)
             src = states[(c, grp)][:, :, local].rearrange("p t (c i) -> p c t i", i=4)
             if (c, grp, piece) == (len(chunks) - 1, PASSES - 1, 1):
                 nc.vector.tensor_copy(out=dst, in_=src)
@@ -300,13 +305,13 @@ def tile_slru_kernel(
             else:
                 nc.scalar.copy(out=dst, in_=src)
 
-        def quantise_x(c, grp):
-            first, n_tokens = chunks[c]
-            tokens = slice(first, first + n_tokens)
+        def quantise_x(c, passes):
+            n_tokens = chunks[c][1]
+            cols = s_cols(c, passes[0], 0, len(passes) * n_tokens)
             nc.vector.quantize_mx(
-                out=s_codes[:, grp, tokens].bitcast(FP8X4),
-                scales=s_scales[:, grp, tokens],
-                in_=grouped_x[(c, grp)][:].rearrange("p r t -> p (r t)"),
+                out=s_codes[:, cols].bitcast(FP8X4),
+                scales=s_scales[:, cols],
+                in_=grouped_x[c][:, passes[0] : passes[-1] + 1, :, :].rearrange("p g r t -> p (g r t)"),
             )
 
         sums = {}
@@ -315,12 +320,13 @@ def tile_slru_kernel(
 
         def second_pass(n, g):
             i, half = divmod(n, FEAT // WIDE)
-            toks = slice(P * i, P * (i + 1))
+            c = chunk_of_pair[i // (PAIR // P)][0]
+            toks = s_cols(c, g, P * i - chunks[c][0], P)
             cols = slice(WIDE * half, WIDE * (half + 1))
             nc.tensor.matmul_mx(
                 out=sums[n][:],
-                lhsT=s_codes[:, g, toks].bitcast(FP8X4),
-                lhsT_scale=s_scales[:, g, toks],
+                lhsT=s_codes[:, toks].bitcast(FP8X4),
+                lhsT_scale=s_scales[:, toks],
                 rhs=wo_codes[half][:, g, :].bitcast(FP8X4),
                 rhs_scale=wo_sc[plane(g) : P, cols],
                 start=(g == 0),
@@ -393,7 +399,10 @@ def tile_slru_kernel(
             c, grp = windows[i]
             done = CHAN_TILES * c + PACK * (grp + 1)
             interleave_at[done] = (c, grp)
-            quantise_x_at[done + (1 if i == len(windows) - 1 else PACK)] = (c, grp)
+            if c == len(chunks) - 1:
+                quantise_x_at[done + (PACK if grp == 0 else 1)] = (c, (grp,))
+            elif grp == PASSES - 1:
+                quantise_x_at[done + PACK] = (c, (0, 1))
 
         for grp in range(PASSES):
             permute_scales(grp)
@@ -418,8 +427,9 @@ def tile_slru_kernel(
             while issued <= min(want, len(scans) - 1):
                 issued += first_layers(scans[issued][0], scans[issued][1])
             if k in quantise_x_at:
-                c, grp = quantise_x_at[k]
-                quantise_x(c, grp)
+                c, passes = quantise_x_at[k]
+                quantise_x(c, passes)
+                grp = passes[-1]
                 if c == len(chunks) - 1:
                     for n in range(n_units - TAIL_UNITS, n_units):
                         if grp == 0:

@@ -25,6 +25,8 @@ TOKENS = BATCH * SEQ
 CHUNK_LENS = (PAIR, PAIR, WIDE, WIDE, PAIR, PAIR)
 assert sum(CHUNK_LENS) == TOKENS
 AHEAD = 2
+WARM_BEFORE = 4
+WARM_BETWEEN = 3
 FLIP_STRIDE = 2
 FLIP_AHEAD = 14
 RESULT_BUFS = 7
@@ -68,6 +70,8 @@ def tile_slru_kernel(
 
         wi_sc_raw = keep.tile([P, CHAN], U8, align_bytes=64)
         nc.vector.memset(wi_sc_raw[:].bitcast(I32), 0)
+        blank = keep.tile([P, WIDE], BF16)
+        nc.vector.memset(blank[:], 0.0)
         wo_sc = keep.tile([P, FEAT], U8, align_bytes=64)
         nc.vector.memset(wo_sc[:].bitcast(I32), 0)
 
@@ -404,6 +408,12 @@ def tile_slru_kernel(
             elif grp == PASSES - 1:
                 quantise_x_at[done + PACK] = (c, (0, 1))
 
+        def keep_busy(n_matmuls):
+            unread = second_psum.tile([P, WIDE], F32, tag="second")
+            for m in range(n_matmuls):
+                nc.tensor.matmul(out=unread[:], lhsT=blank[:, 0:P], rhs=blank[:], start=True, stop=True)
+
+        keep_busy(WARM_BEFORE)
         for grp in range(PASSES):
             permute_scales(grp)
         for g in range(PASSES):
@@ -411,6 +421,7 @@ def tile_slru_kernel(
         for unit in range(chunks[0][1] // PAIR * PASSES):
             flip_inputs(unit)
             quantise_unit(unit)
+        keep_busy(WARM_BETWEEN)
         permute_codes(1, slice(0, PASSES))
         nc.tensor.matmul(out=decay_psum[:], lhsT=ident_f32[:], rhs=decay[:], start=True, stop=True)
         issued = 0

@@ -25,6 +25,7 @@ TOKENS = BATCH * SEQ
 CHUNK_LENS = (PAIR, PAIR, WIDE, WIDE, PAIR, PAIR)
 assert sum(CHUNK_LENS) == TOKENS
 AHEAD = 2
+LAG_FROM = 40
 WARM_BEFORE = 4
 WARM_BETWEEN = 3
 FLIP_STRIDE = 2
@@ -32,7 +33,7 @@ FLIP_AHEAD = 14
 RESULT_BUFS = 7
 GPSIMD_ADDS = 2
 TAIL_UNITS = CHUNK_LENS[-1] // P * (FEAT // WIDE)
-VECTOR_OF_FOUR = (0, 0, 2, 3, 4, 4)
+VECTOR_OF_FOUR = (1, 1, 2, 3, 4, 4)
 GPSIMD_PIECES = (1,)
 
 FLOPS = 2 * BATCH * SEQ * (FEAT * CHAN + CHAN * FEAT)
@@ -463,7 +464,8 @@ def tile_slru_kernel(
                     waiting.remove(n)
             if k in flip_at:
                 flip_inputs(flip_at[k])
-            if added < multiplied:
+            lag = 1 if LAG_FROM <= k < len(scans) else 0
+            if added < multiplied - lag:
                 empty_bank(added)
                 if not on_vector(added):
                     waiting.append(added)

@@ -25,7 +25,7 @@ TOKENS = BATCH * SEQ
 CHUNK_LENS = (PAIR, PAIR, WIDE, WIDE, PAIR, PAIR)
 assert sum(CHUNK_LENS) == TOKENS
 AHEAD = 2
-LAG_FROM = 40
+LAG_FROM = 42
 WARM_BEFORE = 4
 WARM_BETWEEN = 3
 FLIP_STRIDE = 2
@@ -33,7 +33,7 @@ FLIP_AHEAD = 14
 RESULT_BUFS = 7
 GPSIMD_ADDS = 2
 TAIL_UNITS = CHUNK_LENS[-1] // P * (FEAT // WIDE)
-VECTOR_OF_FOUR = (1, 1, 2, 3, 4, 4)
+VECTOR_OF_FOUR = (1, 1, 2, 3, 3, 4)
 GPSIMD_PIECES = (1,)
 
 FLOPS = 2 * BATCH * SEQ * (FEAT * CHAN + CHAN * FEAT)
@@ -55,6 +55,11 @@ def tile_slru_kernel(
         const_psum = ctx.enter_context(tc.psum_pool(name="const_psum", bufs=1))
         second_psum = ctx.enter_context(tc.psum_pool(name="second_psum", bufs=3))
 
+        wi_sc_raw = keep.tile([P, CHAN], U8, align_bytes=64)
+        nc.gpsimd.memset(wi_sc_raw[:].bitcast(I32), 0)
+        ident_f32 = keep.tile([P, P], F32)
+        make_identity(nc, ident_f32[:])
+
         par = keep.tile([P, 3 * PASSES, PACK], BF16)
         nc.scalar.dma_start(
             out=par[:, 0 : 2 * PASSES, :],
@@ -69,8 +74,6 @@ def tile_slru_kernel(
         warm = keep.tile([P, 1], F32)
         nc.scalar.activation(out=warm[:], in_=zero[:], func=ACT.Exp)
 
-        wi_sc_raw = keep.tile([P, CHAN], U8, align_bytes=64)
-        nc.vector.memset(wi_sc_raw[:].bitcast(I32), 0)
         blank = keep.tile([P, WIDE], BF16)
         nc.vector.memset(blank[:], 0.0)
         wo_sc = keep.tile([P, FEAT], U8, align_bytes=64)
@@ -99,8 +102,8 @@ def tile_slru_kernel(
             for grp in range(PASSES)
         ]
         wi_codes = [
-            keep.tile([P, PASSES, K_PASS], U32, align_bytes=64, name="wi_codes%d" % grp)
-            for grp in range(PASSES)
+            keep.tile([P, PASSES, P], U32, align_bytes=64, name="wi_codes%d" % j)
+            for j in range(CHAN_TILES)
         ]
         wi_sc = [
             keep.tile([P, K_PASS], U8, align_bytes=64, name="wi_sc%d" % grp) for grp in range(PASSES)
@@ -117,8 +120,8 @@ def tile_slru_kernel(
                 in_=words.rearrange("g p n t -> p g (n t)").bitcast(I32)[:, passes, cols],
             )
 
-        load_tokens(0, 2)
         load_weight_scales(wi_sc_raw, Wi_scales)
+        load_tokens(0, 2)
         load_weight_codes(wi_raw, Wi_words, 0, slice(0, PASSES))
         load_weight_codes(wi_raw, Wi_words, 1, slice(0, PASSES))
         for pair in range(1, TOKENS // PAIR):
@@ -128,9 +131,6 @@ def tile_slru_kernel(
             load_weight_codes(wo_codes, Wo_words, half, slice(0, PASSES))
         bo_all = keep.tile([P, FEAT], BF16)
         nc.sync.dma_start(out=bo_all[:], in_=bo.partition_broadcast(P))
-
-        ident_f32 = keep.tile([P, P], F32)
-        make_identity(nc, ident_f32[:])
 
         nu = keep.tile([P, CHAN_TILES], F32)
         nc.scalar.activation(
@@ -159,11 +159,10 @@ def tile_slru_kernel(
             for t in range(PACK):
                 nc.vector.tensor_copy(out=wi_sc[grp][:, P * t : P * (t + 1)], in_=raw[:, t, :])
 
-        def permute_codes(grp, passes):
-            nc.vector.tensor_copy(
-                out=wi_codes[grp][:, passes, :].bitcast(I32).rearrange("p g (t m) -> p g t m", t=PACK),
-                in_=wi_raw[grp][:, passes, :].bitcast(I32).rearrange("p g (m t) -> p g t m", t=PACK),
-            )
+        def permute_codes(j):
+            grp, t = divmod(j, PACK)
+            raw = wi_raw[grp][:].bitcast(I32).rearrange("p g (m t) -> p g t m", t=PACK)
+            nc.vector.tensor_copy(out=wi_codes[j][:].bitcast(I32), in_=raw[:, :, t, :])
 
         chunks = []
         for n_tokens in CHUNK_LENS:
@@ -240,7 +239,7 @@ def tile_slru_kernel(
             for g in range(PASSES):
                 nc.tensor.matmul_mx(
                     out=acc,
-                    lhsT=wi_codes[grp][:, g, chans].bitcast(FP8X4),
+                    lhsT=wi_codes[j][:, g, :].bitcast(FP8X4),
                     lhsT_scale=wi_sc[grp][plane(g) : P, chans],
                     rhs=x_codes[:, x_cols(c, g, 0, n_tokens)].bitcast(FP8X4),
                     rhs_scale=x_scales[:, x_cols(c, g, 0, n_tokens)],
@@ -353,7 +352,7 @@ def tile_slru_kernel(
         out_rows = out.rearrange("b s f -> (b s) f")
 
         def on_vector(n):
-            return n % 4 < VECTOR_OF_FOUR[chunk_of_pair[n // (PAIR // P * (FEAT // WIDE))][0]]
+            return n % 4 >= 4 - VECTOR_OF_FOUR[chunk_of_pair[n // (PAIR // P * (FEAT // WIDE))][0]]
 
         def empty_bank(n):
             i, half = divmod(n, FEAT // WIDE)
@@ -417,13 +416,14 @@ def tile_slru_kernel(
         keep_busy(WARM_BEFORE)
         for grp in range(PASSES):
             permute_scales(grp)
-        for g in range(PASSES):
-            permute_codes(0, slice(g, g + 1))
+        for j in range(AHEAD):
+            permute_codes(j)
         for unit in range(chunks[0][1] // PAIR * PASSES):
             flip_inputs(unit)
             quantise_unit(unit)
         keep_busy(WARM_BETWEEN)
-        permute_codes(1, slice(0, PASSES))
+        for j in range(AHEAD, CHAN_TILES):
+            permute_codes(j)
         nc.tensor.matmul(out=decay_psum[:], lhsT=ident_f32[:], rhs=decay[:], start=True, stop=True)
         issued = 0
         while issued < AHEAD:
@@ -459,7 +459,7 @@ def tile_slru_kernel(
                 c, grp = interleave_at[k]
                 interleave_x(c, grp, 0)
                 interleave_x(c, grp, 1)
-                for n in waiting[:GPSIMD_ADDS]:
+                for n in waiting[: GPSIMD_ADDS if k < max(interleave_at) else n_units]:
                     gpsimd_add(n)
                     waiting.remove(n)
             if k in flip_at:
@@ -468,7 +468,10 @@ def tile_slru_kernel(
             if added < multiplied - lag:
                 empty_bank(added)
                 if not on_vector(added):
-                    waiting.append(added)
+                    if k < max(interleave_at):
+                        waiting.append(added)
+                    else:
+                        gpsimd_add(added)
                 added += 1
             if multiplied < ready:
                 second_matmul(multiplied)

@@ -31,7 +31,7 @@ WARM_BETWEEN = 3
 FLIP_STRIDE = 2
 FLIP_AHEAD = 14
 RESULT_BUFS = 7
-GPSIMD_ADDS = 2
+ADD_STEPS = (5, 7, 1)
 TAIL_UNITS = CHUNK_LENS[-1] // P * (FEAT // WIDE)
 VECTOR_OF_FOUR = (1, 1, 2, 3, 3, 4)
 GPSIMD_PIECES = (1,)
@@ -64,10 +64,6 @@ def tile_slru_kernel(
         nc.scalar.dma_start(
             out=par[:, 0 : 2 * PASSES, :],
             in_=params_log.rearrange("r (g p t) -> p (r g) t", p=P, t=PACK),
-        )
-        nc.gpsimd.dma_start(
-            out=par[:, 2 * PASSES : 3 * PASSES, :],
-            in_=bi.rearrange("(g p t) -> p g t", p=P, t=PACK),
         )
         zero = keep.tile([P, 1], F32)
         nc.vector.memset(zero[:], 0.0)
@@ -124,6 +120,10 @@ def tile_slru_kernel(
         load_tokens(0, 2)
         load_weight_codes(wi_raw, Wi_words, 0, slice(0, PASSES))
         load_weight_codes(wi_raw, Wi_words, 1, slice(0, PASSES))
+        nc.sync.dma_start(
+            out=par[:, 2 * PASSES : 3 * PASSES, :],
+            in_=bi.rearrange("(g p t) -> p g t", p=P, t=PACK),
+        )
         for pair in range(1, TOKENS // PAIR):
             load_tokens(2 * pair, 2)
         load_weight_scales(wo_sc, Wo_scales)
@@ -375,16 +375,10 @@ def tile_slru_kernel(
             )
             finish(n)
 
-        finished = set()
-
         def finish(n):
             i, half = divmod(n, FEAT // WIDE)
             cols = slice(WIDE * half, WIDE * (half + 1))
-            finished.add(n)
-            if n >= n_units - TAIL_UNITS:
-                nc.sync.dma_start(out=out_rows[P * i : P * (i + 1), cols], in_=results[i][:, cols])
-            elif all(m in finished for m in range(i * (FEAT // WIDE), (i + 1) * (FEAT // WIDE))):
-                nc.sync.dma_start(out=out_rows[P * i : P * (i + 1), :], in_=results[i][:])
+            nc.sync.dma_start(out=out_rows[P * i : P * (i + 1), cols], in_=results[i][:, cols])
 
         scans = [(c, j) for c in range(len(chunks)) for j in range(CHAN_TILES)]
         flip_at = {}
@@ -433,11 +427,6 @@ def tile_slru_kernel(
         added = 0
         waiting = []
         for k in range(len(scans) + n_units):
-            if k in quantise_in_at:
-                quantise_chunk(quantise_in_at[k])
-            want = k + AHEAD + (1 if k in interleave_at else 0)
-            while issued <= min(want, len(scans) - 1):
-                issued += first_layers(scans[issued][0], scans[issued][1])
             if k in quantise_x_at:
                 c, passes = quantise_x_at[k]
                 quantise_x(c, passes)
@@ -453,25 +442,27 @@ def tile_slru_kernel(
                         multiplied = n_units
                 elif grp == PASSES - 1:
                     ready += chunks[c][1] // P * (FEAT // WIDE)
+            if k in quantise_in_at:
+                quantise_chunk(quantise_in_at[k])
+            want = k + AHEAD + (1 if k in interleave_at else 0)
+            while issued <= min(want, len(scans) - 1):
+                issued += first_layers(scans[issued][0], scans[issued][1])
             if k < len(scans):
                 recurrence(scans[k][0], scans[k][1])
             if k in interleave_at:
                 c, grp = interleave_at[k]
                 interleave_x(c, grp, 0)
                 interleave_x(c, grp, 1)
-                for n in waiting[: GPSIMD_ADDS if k < max(interleave_at) else n_units]:
-                    gpsimd_add(n)
-                    waiting.remove(n)
+            if waiting and (k % CHAN_TILES in ADD_STEPS or k >= max(interleave_at)):
+                gpsimd_add(waiting[0])
+                waiting = waiting[1:]
             if k in flip_at:
                 flip_inputs(flip_at[k])
             lag = 1 if LAG_FROM <= k < len(scans) else 0
             if added < multiplied - lag:
                 empty_bank(added)
                 if not on_vector(added):
-                    if k < max(interleave_at):
-                        waiting.append(added)
-                    else:
-                        gpsimd_add(added)
+                    waiting.append(added)
                 added += 1
             if multiplied < ready:
                 second_matmul(multiplied)

@@ -28,12 +28,12 @@ AHEAD = 2
 LAG_FROM = 42
 WARM_BEFORE = 4
 WARM_BETWEEN = 3
-FLIP_STRIDE = 2
-FLIP_AHEAD = 14
+FLIP_STRIDE = 4
+FLIP_AHEAD = 12
 RESULT_BUFS = 7
 ADD_STEPS = (5, 7, 1)
 TAIL_UNITS = CHUNK_LENS[-1] // P * (FEAT // WIDE)
-VECTOR_OF_FOUR = (1, 1, 2, 3, 3, 4)
+VECTOR_OF_FOUR = (1, 1, 2, 2, 4, 4)
 GPSIMD_PIECES = (1,)
 
 FLOPS = 2 * BATCH * SEQ * (FEAT * CHAN + CHAN * FEAT)
@@ -55,21 +55,22 @@ def tile_slru_kernel(
         const_psum = ctx.enter_context(tc.psum_pool(name="const_psum", bufs=1))
         second_psum = ctx.enter_context(tc.psum_pool(name="second_psum", bufs=3))
 
-        wi_sc_raw = keep.tile([P, CHAN], U8, align_bytes=64)
-        nc.gpsimd.memset(wi_sc_raw[:].bitcast(I32), 0)
-        ident_f32 = keep.tile([P, P], F32)
-        make_identity(nc, ident_f32[:])
-
         par = keep.tile([P, 3 * PASSES, PACK], BF16)
         nc.scalar.dma_start(
             out=par[:, 0 : 2 * PASSES, :],
             in_=params_log.rearrange("r (g p t) -> p (r g) t", p=P, t=PACK),
+        )
+        nc.gpsimd.dma_start(
+            out=par[:, 2 * PASSES : 3 * PASSES, :],
+            in_=bi.rearrange("(g p t) -> p g t", p=P, t=PACK),
         )
         zero = keep.tile([P, 1], F32)
         nc.vector.memset(zero[:], 0.0)
         warm = keep.tile([P, 1], F32)
         nc.scalar.activation(out=warm[:], in_=zero[:], func=ACT.Exp)
 
+        wi_sc_raw = keep.tile([P, CHAN], U8, align_bytes=64)
+        nc.vector.memset(wi_sc_raw[:].bitcast(I32), 0)
         blank = keep.tile([P, WIDE], BF16)
         nc.vector.memset(blank[:], 0.0)
         wo_sc = keep.tile([P, FEAT], U8, align_bytes=64)
@@ -116,14 +117,10 @@ def tile_slru_kernel(
                 in_=words.rearrange("g p n t -> p g (n t)").bitcast(I32)[:, passes, cols],
             )
 
-        load_weight_scales(wi_sc_raw, Wi_scales)
         load_tokens(0, 2)
+        load_weight_scales(wi_sc_raw, Wi_scales)
         load_weight_codes(wi_raw, Wi_words, 0, slice(0, PASSES))
         load_weight_codes(wi_raw, Wi_words, 1, slice(0, PASSES))
-        nc.sync.dma_start(
-            out=par[:, 2 * PASSES : 3 * PASSES, :],
-            in_=bi.rearrange("(g p t) -> p g t", p=P, t=PACK),
-        )
         for pair in range(1, TOKENS // PAIR):
             load_tokens(2 * pair, 2)
         load_weight_scales(wo_sc, Wo_scales)
@@ -131,6 +128,9 @@ def tile_slru_kernel(
             load_weight_codes(wo_codes, Wo_words, half, slice(0, PASSES))
         bo_all = keep.tile([P, FEAT], BF16)
         nc.sync.dma_start(out=bo_all[:], in_=bo.partition_broadcast(P))
+
+        ident_f32 = keep.tile([P, P], F32)
+        make_identity(nc, ident_f32[:])
 
         nu = keep.tile([P, CHAN_TILES], F32)
         nc.scalar.activation(
@@ -180,28 +180,33 @@ def tile_slru_kernel(
             start = PASSES * chunks[c][0] + g * chunks[c][1] + first
             return slice(start, start + n_cols)
 
-        def flip_inputs(unit):
-            pair, g = divmod(unit, PASSES)
-            c, h = chunk_of_pair[pair]
-            if (h, g) == (0, 0):
-                grouped_in[c] = wide.tile(
-                    [P, PASSES, chunks[c][1] * PACK], BF16, align_bytes=64, name="gin%d" % c, tag="grouped_in"
-                )
-            flipped = flip_psum.tile([P, 2, PAIR], F32, tag="flip")
-            for i in range(2):
-                words = x_rows[:, 2 * pair + i, :].bitcast(F32)
-                for u in range(2):
-                    nc.tensor.transpose(
-                        flipped[:, u, P * i : P * (i + 1)],
-                        words[:, 2 * P * g + u : 2 * P * (g + 1) : 2],
-                        ident_f32[:],
+        def flip_inputs(first, n_units):
+            flipped = {}
+            for unit in range(first, first + n_units):
+                pair, g = divmod(unit, PASSES)
+                c, h = chunk_of_pair[pair]
+                if (h, g) == (0, 0):
+                    grouped_in[c] = wide.tile(
+                        [P, PASSES, chunks[c][1] * PACK], BF16, align_bytes=64, name="gin%d" % c, tag="grouped_in"
                     )
-            nc.scalar.copy(
-                out=grouped_in[c][:, g, PAIR * PACK * h : PAIR * PACK * (h + 1)]
-                .bitcast(F32)
-                .rearrange("p (r u) -> p r u", u=2),
-                in_=flipped[:].rearrange("p u r -> p r u"),
-            )
+                flipped[unit] = flip_psum.tile([P, 2, PAIR], F32, name="flip%d" % unit, tag="flip")
+                for i in range(2):
+                    words = x_rows[:, 2 * pair + i, :].bitcast(F32)
+                    for u in range(2):
+                        nc.tensor.transpose(
+                            flipped[unit][:, u, P * i : P * (i + 1)],
+                            words[:, 2 * P * g + u : 2 * P * (g + 1) : 2],
+                            ident_f32[:],
+                        )
+            for unit in range(first, first + n_units):
+                pair, g = divmod(unit, PASSES)
+                c, h = chunk_of_pair[pair]
+                nc.scalar.copy(
+                    out=grouped_in[c][:, g, PAIR * PACK * h : PAIR * PACK * (h + 1)]
+                    .bitcast(F32)
+                    .rearrange("p (r u) -> p r u", u=2),
+                    in_=flipped[unit][:].rearrange("p u r -> p r u"),
+                )
 
         def quantise_unit(unit):
             pair, g = divmod(unit, PASSES)
@@ -386,11 +391,10 @@ def tile_slru_kernel(
         interleave_at = {}
         quantise_x_at = {}
         for c in range(1, len(chunks)):
-            first_step = CHAN_TILES * c - FLIP_AHEAD
-            for a in range(chunks[c][1] // PAIR * PASSES):
-                step = a if first_step < 0 else first_step + FLIP_STRIDE * a
+            for h in range(chunks[c][1] // PAIR):
+                step = max(CHAN_TILES * c - FLIP_AHEAD + FLIP_STRIDE * h, 0)
                 assert step not in flip_at
-                flip_at[step] = chunks[c][0] // PAIR * PASSES + a
+                flip_at[step] = chunks[c][0] // PAIR + h
             quantise_in_at[CHAN_TILES * c - PACK] = c
         windows = [(c, grp) for c in range(len(chunks)) for grp in range(PASSES)]
         for i in range(len(windows)):
@@ -413,7 +417,7 @@ def tile_slru_kernel(
         for j in range(AHEAD):
             permute_codes(j)
         for unit in range(chunks[0][1] // PAIR * PASSES):
-            flip_inputs(unit)
+            flip_inputs(unit, 1)
             quantise_unit(unit)
         keep_busy(WARM_BETWEEN)
         for j in range(AHEAD, CHAN_TILES):
@@ -457,7 +461,7 @@ def tile_slru_kernel(
                 gpsimd_add(waiting[0])
                 waiting = waiting[1:]
             if k in flip_at:
-                flip_inputs(flip_at[k])
+                flip_inputs(PASSES * flip_at[k], PASSES)
             lag = 1 if LAG_FROM <= k < len(scans) else 0
             if added < multiplied - lag:
                 empty_bank(added)

@@ -31,9 +31,10 @@ WARM_BETWEEN = 3
 FLIP_STRIDE = 4
 FLIP_AHEAD = 12
 RESULT_BUFS = 7
-ADD_STEPS = (5, 7, 1)
+ADD_STEPS = (5, 7, 0, 2)
 TAIL_UNITS = CHUNK_LENS[-1] // P * (FEAT // WIDE)
-VECTOR_OF_FOUR = (1, 1, 2, 2, 4, 4)
+VECTOR_OF_FOUR = (1, 1, 1, 2, 4, 4)
+SCALAR_EIGHTHS = ((0, 4), (4, 6))
 GPSIMD_PIECES = (1,)
 
 FLOPS = 2 * BATCH * SEQ * (FEAT * CHAN + CHAN * FEAT)
@@ -298,16 +299,19 @@ def tile_slru_kernel(
 
         def interleave_x(c, grp, piece):
             n_tokens = chunks[c][1]
-            local = slice(piece * n_tokens // 2, (piece + 1) * n_tokens // 2)
+            cut = n_tokens * SCALAR_EIGHTHS[min(c // 2, 1)][grp] // 8
+            local = slice(0, cut) if piece == 0 else slice(cut, n_tokens)
             if (grp, piece) == (0, 0):
                 grouped_x[c] = single.tile(
                     [P, PASSES, n_tokens, PACK], BF16, align_bytes=64, name="gx%d" % c, tag="grouped_x"
                 )
+            if local.start == local.stop:
+                return
             dst = grouped_x[c][:, grp, local, :].rearrange("p (c i) t -> p c t i", i=4)
             src = states[(c, grp)][:, :, local].rearrange("p t (c i) -> p c t i", i=4)
             if (c, grp, piece) == (len(chunks) - 1, PASSES - 1, 1):
                 nc.vector.tensor_copy(out=dst, in_=src)
-            elif piece in (GPSIMD_PIECES if c >= 2 else (0, 1)):
+            elif piece in GPSIMD_PIECES:
                 nc.gpsimd.tensor_scalar(
                     out=dst, in0=src, scalar1=1.0, scalar2=0.0, op0=ALU.mult, op1=ALU.add
                 )

@@ -28,12 +28,13 @@ AHEAD = 2
 LAG_FROM = 42
 WARM_BEFORE = 4
 WARM_BETWEEN = 3
+PERMUTED = ((0, 2), (2, 2), (4, 4))
 FLIP_STRIDE = 4
 FLIP_AHEAD = 12
 RESULT_BUFS = 7
-ADD_STEPS = (5, 7, 0, 2)
+ADD_STEPS = (5, 7, 0)
 TAIL_UNITS = CHUNK_LENS[-1] // P * (FEAT // WIDE)
-VECTOR_OF_FOUR = (1, 1, 1, 2, 4, 4)
+VECTOR_OF_FOUR = (1, 1, 2, 2, 4, 4)
 SCALAR_EIGHTHS = ((0, 4), (4, 6))
 GPSIMD_PIECES = (1,)
 
@@ -100,8 +101,8 @@ def tile_slru_kernel(
             for grp in range(PASSES)
         ]
         wi_codes = [
-            keep.tile([P, PASSES, P], U32, align_bytes=64, name="wi_codes%d" % j)
-            for j in range(CHAN_TILES)
+            keep.tile([P, n_tiles, PASSES, P], U32, align_bytes=64, name="wi_codes%d" % first)
+            for first, n_tiles in PERMUTED
         ]
         wi_sc = [
             keep.tile([P, K_PASS], U8, align_bytes=64, name="wi_sc%d" % grp) for grp in range(PASSES)
@@ -160,10 +161,17 @@ def tile_slru_kernel(
             for t in range(PACK):
                 nc.vector.tensor_copy(out=wi_sc[grp][:, P * t : P * (t + 1)], in_=raw[:, t, :])
 
-        def permute_codes(j):
-            grp, t = divmod(j, PACK)
-            raw = wi_raw[grp][:].bitcast(I32).rearrange("p g (m t) -> p g t m", t=PACK)
-            nc.vector.tensor_copy(out=wi_codes[j][:].bitcast(I32), in_=raw[:, :, t, :])
+        def permute_codes(part):
+            first, n_tiles = PERMUTED[part]
+            grp, t = divmod(first, PACK)
+            raw = wi_raw[grp][:].bitcast(I32).rearrange("p g (m t) -> p t g m", t=PACK)
+            nc.vector.tensor_copy(out=wi_codes[part][:].bitcast(I32), in_=raw[:, t : t + n_tiles, :, :])
+
+        part_of = {
+            first + i: (part, i)
+            for part, (first, n_tiles) in enumerate(PERMUTED)
+            for i in range(n_tiles)
+        }
 
         chunks = []
         for n_tokens in CHUNK_LENS:
@@ -245,7 +253,7 @@ def tile_slru_kernel(
             for g in range(PASSES):
                 nc.tensor.matmul_mx(
                     out=acc,
-                    lhsT=wi_codes[j][:, g, :].bitcast(FP8X4),
+                    lhsT=wi_codes[part_of[j][0]][:, part_of[j][1], g, :].bitcast(FP8X4),
                     lhsT_scale=wi_sc[grp][plane(g) : P, chans],
                     rhs=x_codes[:, x_cols(c, g, 0, n_tokens)].bitcast(FP8X4),
                     rhs_scale=x_scales[:, x_cols(c, g, 0, n_tokens)],
@@ -418,14 +426,13 @@ def tile_slru_kernel(
         keep_busy(WARM_BEFORE)
         for grp in range(PASSES):
             permute_scales(grp)
-        for j in range(AHEAD):
-            permute_codes(j)
+        permute_codes(0)
         for unit in range(chunks[0][1] // PAIR * PASSES):
             flip_inputs(unit, 1)
             quantise_unit(unit)
         keep_busy(WARM_BETWEEN)
-        for j in range(AHEAD, CHAN_TILES):
-            permute_codes(j)
+        for part in range(1, len(PERMUTED)):
+            permute_codes(part)
         nc.tensor.matmul(out=decay_psum[:], lhsT=ident_f32[:], rhs=decay[:], start=True, stop=True)
         issued = 0
         while issued < AHEAD:

from contextlib import ExitStack

import concourse.mybir as mybir
from concourse.masks import make_identity

F32 = mybir.dt.float32
BF16 = mybir.dt.bfloat16
I32 = mybir.dt.int32
U32 = mybir.dt.uint32
U8 = mybir.dt.uint8
FP8X4 = mybir.dt.float8_e4m3fn_x4
ACT = mybir.ActivationFunctionType
ALU = mybir.AluOpType

BATCH, SEQ, FEAT, CHAN = 2, 1024, 1024, 1024

P = 128
PACK = 4
K_PASS = P * PACK
PASSES = FEAT // K_PASS
WIDE = 512
CHAN_TILES = CHAN // P
PAIR = 2 * P
TOKENS = BATCH * SEQ
CHUNK_LENS = (PAIR, PAIR, WIDE, WIDE, PAIR, PAIR)
assert sum(CHUNK_LENS) == TOKENS
AHEAD = 2
LAG_FROM = 42
WARM_BEFORE = 4
WARM_BETWEEN = 3
PERMUTED = ((0, 2), (2, 2), (4, 4))
FLIP_STRIDE = 4
FLIP_AHEAD = 12
RESULT_BUFS = 7
ADD_STEPS = (5, 7, 0)
TAIL_UNITS = CHUNK_LENS[-1] // P * (FEAT // WIDE)
VECTOR_OF_FOUR = (1, 1, 2, 2, 4, 4)
SCALAR_EIGHTHS = ((0, 4), (4, 6))
GPSIMD_PIECES = (1,)

FLOPS = 2 * BATCH * SEQ * (FEAT * CHAN + CHAN * FEAT)


def tile_slru_kernel(
    tc, inputs, Wi_words, Wi_scales, bi, Wo_words, Wo_scales, bo, params_log, out
):
    nc = tc.nc
    with ExitStack() as ctx:
        ctx.enter_context(tc.manual_schedule())
        keep = ctx.enter_context(tc.tile_pool(name="keep", bufs=1))
        stream = ctx.enter_context(tc.tile_pool(name="stream", bufs=4))
        wide = ctx.enter_context(tc.tile_pool(name="wide", bufs=2))
        single = ctx.enter_context(tc.tile_pool(name="single", bufs=1))
        rows_pool = ctx.enter_context(tc.tile_pool(name="rows_pool", bufs=RESULT_BUFS))
        flip_psum = ctx.enter_context(tc.psum_pool(name="flip_psum", bufs=2))
        first_psum = ctx.enter_context(tc.psum_pool(name="first_psum", bufs=2))
        const_psum = ctx.enter_context(tc.psum_pool(name="const_psum", bufs=1))
        second_psum = ctx.enter_context(tc.psum_pool(name="second_psum", bufs=3))

        par = keep.tile([P, 3 * PASSES, PACK], BF16)
        nc.scalar.dma_start(
            out=par[:, 0 : 2 * PASSES, :],
            in_=params_log.rearrange("r (g p t) -> p (r g) t", p=P, t=PACK),
        )
        nc.gpsimd.dma_start(
            out=par[:, 2 * PASSES : 3 * PASSES, :],
            in_=bi.rearrange("(g p t) -> p g t", p=P, t=PACK),
        )
        zero = keep.tile([P, 1], F32)
        nc.vector.memset(zero[:], 0.0)
        warm = keep.tile([P, 1], F32)
        nc.scalar.activation(out=warm[:], in_=zero[:], func=ACT.Exp)

        wi_sc_raw = keep.tile([P, CHAN], U8, align_bytes=64)
        nc.vector.memset(wi_sc_raw[:].bitcast(I32), 0)
        blank = keep.tile([P, WIDE], BF16)
        nc.vector.memset(blank[:], 0.0)
        wo_sc = keep.tile([P, FEAT], U8, align_bytes=64)
        nc.vector.memset(wo_sc[:].bitcast(I32), 0)

        def plane(g):
            return PACK * g

        def load_weight_scales(planes, scales):
            for quad in range(4):
                top = 32 * quad
                nc.sync.dma_start(
                    out=planes[top : top + PACK * PASSES, :].bitcast(I32),
                    in_=scales.bitcast(I32)[:, 4 * quad : 4 * quad + 4, :],
                )

        x_rows = keep.tile([P, TOKENS // P, FEAT], BF16)
        x_dram = inputs.rearrange("b (i p) f -> p (b i) f", p=P)

        def load_tokens(first_tile, n_tiles):
            tiles = slice(first_tile, first_tile + n_tiles)
            nc.sync.dma_start(out=x_rows[:, tiles, :], in_=x_dram[:, tiles, :])

        wi_raw = [
            keep.tile([P, PASSES, K_PASS], U32, align_bytes=64, name="wi_raw%d" % grp)
            for grp in range(PASSES)
        ]
        wi_codes = [
            keep.tile([P, n_tiles, PASSES, P], U32, align_bytes=64, name="wi_codes%d" % first)
            for first, n_tiles in PERMUTED
        ]
        wi_sc = [
            keep.tile([P, K_PASS], U8, align_bytes=64, name="wi_sc%d" % grp) for grp in range(PASSES)
        ]
        wo_codes = [
            keep.tile([P, PASSES, WIDE], U32, align_bytes=64, name="wo_codes%d" % half)
            for half in range(FEAT // WIDE)
        ]

        def load_weight_codes(codes, words, part, passes):
            cols = slice(K_PASS * part, K_PASS * (part + 1))
            nc.sync.dma_start(
                out=codes[part][:, passes, :].bitcast(I32),
                in_=words.rearrange("g p n t -> p g (n t)").bitcast(I32)[:, passes, cols],
            )

        load_tokens(0, 2)
        load_weight_scales(wi_sc_raw, Wi_scales)
        load_weight_codes(wi_raw, Wi_words, 0, slice(0, PASSES))
        load_weight_codes(wi_raw, Wi_words, 1, slice(0, PASSES))
        for pair in range(1, TOKENS // PAIR):
            load_tokens(2 * pair, 2)
        load_weight_scales(wo_sc, Wo_scales)
        for half in range(FEAT // WIDE):
            load_weight_codes(wo_codes, Wo_words, half, slice(0, PASSES))
        bo_all = keep.tile([P, FEAT], BF16)
        nc.sync.dma_start(out=bo_all[:], in_=bo.partition_broadcast(P))

        ident_f32 = keep.tile([P, P], F32)
        make_identity(nc, ident_f32[:])

        nu = keep.tile([P, CHAN_TILES], F32)
        nc.scalar.activation(
            out=nu[:], in_=par[:, 0:PASSES, :].rearrange("p g t -> p (g t)"), func=ACT.Exp
        )
        decay = keep.tile([P, CHAN_TILES], F32)
        nc.scalar.activation(out=decay[:], in_=nu[:], func=ACT.Exp, scale=-1.0)
        decay_psum = const_psum.tile([P, CHAN_TILES], F32)
        gamma = keep.tile([P, CHAN_TILES], F32)
        nc.scalar.activation(
            out=gamma[:],
            in_=par[:, PASSES : 2 * PASSES, :].rearrange("p g t -> p (g t)"),
            func=ACT.Exp,
        )
        gamma_bi = keep.tile([P, CHAN_TILES], F32)
        nc.gpsimd.tensor_tensor(
            out=gamma_bi[:],
            in0=gamma[:],
            in1=par[:, 2 * PASSES : 3 * PASSES, :].rearrange("p g t -> p (g t)"),
            op=ALU.mult,
        )

        def permute_scales(grp):
            cols = slice(K_PASS * grp, K_PASS * (grp + 1))
            raw = wi_sc_raw[:, cols].rearrange("p (m t) -> p t m", t=PACK)
            for t in range(PACK):
                nc.vector.tensor_copy(out=wi_sc[grp][:, P * t : P * (t + 1)], in_=raw[:, t, :])

        def permute_codes(part):
            first, n_tiles = PERMUTED[part]
            grp, t = divmod(first, PACK)
            raw = wi_raw[grp][:].bitcast(I32).rearrange("p g (m t) -> p t g m", t=PACK)
            nc.vector.tensor_copy(out=wi_codes[part][:].bitcast(I32), in_=raw[:, t : t + n_tiles, :, :])

        part_of = {
            first + i: (part, i)
            for part, (first, n_tiles) in enumerate(PERMUTED)
            for i in range(n_tiles)
        }

        chunks = []
        for n_tokens in CHUNK_LENS:
            chunks.append((sum(CHUNK_LENS[: len(chunks)]), n_tokens))
        chunk_of_pair = {}
        for c in range(len(chunks)):
            for h in range(chunks[c][1] // PAIR):
                chunk_of_pair[chunks[c][0] // PAIR + h] = (c, h)

        x_codes = keep.tile([P, PASSES * TOKENS], U32, align_bytes=64)
        x_scales = keep.tile([P, PASSES * TOKENS], U8, align_bytes=64)
        grouped_in = {}

        def x_cols(c, g, first, n_cols):
            start = PASSES * chunks[c][0] + g * chunks[c][1] + first
            return slice(start, start + n_cols)

        def flip_inputs(first, n_units):
            flipped = {}
            for unit in range(first, first + n_units):
                pair, g = divmod(unit, PASSES)
                c, h = chunk_of_pair[pair]
                if (h, g) == (0, 0):
                    grouped_in[c] = wide.tile(
                        [P, PASSES, chunks[c][1] * PACK], BF16, align_bytes=64, name="gin%d" % c, tag="grouped_in"
                    )
                flipped[unit] = flip_psum.tile([P, 2, PAIR], F32, name="flip%d" % unit, tag="flip")
                for i in range(2):
                    words = x_rows[:, 2 * pair + i, :].bitcast(F32)
                    for u in range(2):
                        nc.tensor.transpose(
                            flipped[unit][:, u, P * i : P * (i + 1)],
                            words[:, 2 * P * g + u : 2 * P * (g + 1) : 2],
                            ident_f32[:],
                        )
            for unit in range(first, first + n_units):
                pair, g = divmod(unit, PASSES)
                c, h = chunk_of_pair[pair]
                nc.scalar.copy(
                    out=grouped_in[c][:, g, PAIR * PACK * h : PAIR * PACK * (h + 1)]
                    .bitcast(F32)
                    .rearrange("p (r u) -> p r u", u=2),
                    in_=flipped[unit][:].rearrange("p u r -> p r u"),
                )

        def quantise_unit(unit):
            pair, g = divmod(unit, PASSES)
            c, h = chunk_of_pair[pair]
            nc.vector.quantize_mx(
                out=x_codes[:, x_cols(c, g, PAIR * h, PAIR)].bitcast(FP8X4),
                scales=x_scales[:, x_cols(c, g, PAIR * h, PAIR)],
                in_=grouped_in[c][:, g, PAIR * PACK * h : PAIR * PACK * (h + 1)],
            )

        def quantise_chunk(c):
            cols = x_cols(c, 0, 0, PASSES * chunks[c][1])
            nc.vector.quantize_mx(
                out=x_codes[:, cols].bitcast(FP8X4),
                scales=x_scales[:, cols],
                in_=grouped_in[c][:].rearrange("p g n -> p (g n)"),
            )

        drives = {}

        def first_layers(c, j):
            n_tokens = chunks[c][1]
            sums_in = first_psum.tile([P, WIDE], F32, name="first%d_%d" % (c, j), tag="first")
            parts = [sums_in[:, n_tokens * i : n_tokens * (i + 1)] for i in range(WIDE // n_tokens)]
            for i in range(len(parts)):
                multiply_first(c, j + i, parts[i])
            for i in range(len(parts)):
                drive_scan(c, j + i, parts[i])
            return len(parts)

        def multiply_first(c, j, acc):
            grp, t = divmod(j, PACK)
            chans = slice(P * t, P * (t + 1))
            n_tokens = chunks[c][1]
            for g in range(PASSES):
                nc.tensor.matmul_mx(
                    out=acc,
                    lhsT=wi_codes[part_of[j][0]][:, part_of[j][1], g, :].bitcast(FP8X4),
                    lhsT_scale=wi_sc[grp][plane(g) : P, chans],
                    rhs=x_codes[:, x_cols(c, g, 0, n_tokens)].bitcast(FP8X4),
                    rhs_scale=x_scales[:, x_cols(c, g, 0, n_tokens)],
                    start=(g == 0),
                    stop=(g == PASSES - 1),
                )

        def drive_scan(c, j, acc):
            n_tokens = chunks[c][1]
            drive = stream.tile([P, WIDE], F32, tag="drive")
            nc.scalar.activation(
                out=drive[:, 0:n_tokens],
                in_=acc,
                func=ACT.Identity,
                scale=gamma[:, j : j + 1],
                bias=gamma_bi[:, j : j + 1],
            )
            drives[(c, j)] = drive

        states = {}

        def recurrence(c, j):
            first, n_tokens = chunks[c]
            grp, t = divmod(j, PACK)
            if t == 0:
                states[(c, grp)] = stream.tile(
                    [P, PACK, WIDE], F32, name="state%d_%d" % (c, grp), tag="state"
                )
            if first % SEQ == 0:
                carry = 0.0
            else:
                last = chunks[c - 1][1] - 1
                carry = states[(c - 1, grp)][:, t, last : last + 1]
            nc.vector.tensor_tensor_scan(
                out=states[(c, grp)][:, t, 0:n_tokens],
                data0=decay_psum[:, j : j + 1].to_broadcast([P, n_tokens]),
                data1=drives[(c, j)][:, 0:n_tokens],
                initial=carry,
                op0=ALU.mult,
                op1=ALU.add,
            )

        s_codes = keep.tile([P, PASSES * TOKENS], U32, align_bytes=64)
        s_scales = keep.tile([P, PASSES * TOKENS], U8, align_bytes=64)

        def s_cols(c, g, first, n_tokens):
            start = PASSES * chunks[c][0] + g * chunks[c][1] + first
            return slice(start, start + n_tokens)

        grouped_x = {}

        def interleave_x(c, grp, piece):
            n_tokens = chunks[c][1]
            cut = n_tokens * SCALAR_EIGHTHS[min(c // 2, 1)][grp] // 8
            local = slice(0, cut) if piece == 0 else slice(cut, n_tokens)
            if (grp, piece) == (0, 0):
                grouped_x[c] = single.tile(
                    [P, PASSES, n_tokens, PACK], BF16, align_bytes=64, name="gx%d" % c, tag="grouped_x"
                )
            if local.start == local.stop:
                return
            dst = grouped_x[c][:, grp, local, :].rearrange("p (c i) t -> p c t i", i=4)
            src = states[(c, grp)][:, :, local].rearrange("p t (c i) -> p c t i", i=4)
            if (c, grp, piece) == (len(chunks) - 1, PASSES - 1, 1):
                nc.vector.tensor_copy(out=dst, in_=src)
            elif piece in GPSIMD_PIECES:
                nc.gpsimd.tensor_scalar(
                    out=dst, in0=src, scalar1=1.0, scalar2=0.0, op0=ALU.mult, op1=ALU.add
                )
            else:
                nc.scalar.copy(out=dst, in_=src)

        def quantise_x(c, passes):
            n_tokens = chunks[c][1]
            cols = s_cols(c, passes[0], 0, len(passes) * n_tokens)
            nc.vector.quantize_mx(
                out=s_codes[:, cols].bitcast(FP8X4),
                scales=s_scales[:, cols],
                in_=grouped_x[c][:, passes[0] : passes[-1] + 1, :, :].rearrange("p g r t -> p (g r t)"),
            )

        sums = {}
        results = {}
        n_units = TOKENS // P * (FEAT // WIDE)

        def second_pass(n, g):
            i, half = divmod(n, FEAT // WIDE)
            c = chunk_of_pair[i // (PAIR // P)][0]
            toks = s_cols(c, g, P * i - chunks[c][0], P)
            cols = slice(WIDE * half, WIDE * (half + 1))
            nc.tensor.matmul_mx(
                out=sums[n][:],
                lhsT=s_codes[:, toks].bitcast(FP8X4),
                lhsT_scale=s_scales[:, toks],
                rhs=wo_codes[half][:, g, :].bitcast(FP8X4),
                rhs_scale=wo_sc[plane(g) : P, cols],
                start=(g == 0),
                stop=(g == PASSES - 1),
            )

        def second_matmul(n):
            sums[n] = second_psum.tile([P, WIDE], F32, name="sum%d" % n, tag="second")
            for g in range(PASSES):
                second_pass(n, g)

        def open_tail(n):
            if n % 2 == 0:
                sums[n] = first_psum.tile([P, WIDE], F32, name="sum%d" % n, tag="first")
            else:
                sums[n] = flip_psum.tile([P, WIDE], F32, name="sum%d" % n, tag="flip")
            second_pass(n, 0)

        out_rows = out.rearrange("b s f -> (b s) f")

        def on_vector(n):
            return n % 4 >= 4 - VECTOR_OF_FOUR[chunk_of_pair[n // (PAIR // P * (FEAT // WIDE))][0]]

        def empty_bank(n):
            i, half = divmod(n, FEAT // WIDE)
            cols = slice(WIDE * half, WIDE * (half + 1))
            if half == 0:
                results[i] = rows_pool.tile([P, FEAT], F32, name="result%d" % i, tag="result")
            if on_vector(n):
                nc.vector.tensor_tensor(
                    out=results[i][:, cols], in0=sums[n][:], in1=bo_all[:, cols], op=ALU.add
                )
                finish(n)
            else:
                nc.scalar.copy(out=results[i][:, cols], in_=sums[n][:])

        def gpsimd_add(n):
            i, half = divmod(n, FEAT // WIDE)
            cols = slice(WIDE * half, WIDE * (half + 1))
            nc.gpsimd.tensor_tensor(
                out=results[i][:, cols], in0=results[i][:, cols], in1=bo_all[:, cols], op=ALU.add
            )
            finish(n)

        def finish(n):
            i, half = divmod(n, FEAT // WIDE)
            cols = slice(WIDE * half, WIDE * (half + 1))
            nc.sync.dma_start(out=out_rows[P * i : P * (i + 1), cols], in_=results[i][:, cols])

        scans = [(c, j) for c in range(len(chunks)) for j in range(CHAN_TILES)]
        flip_at = {}
        quantise_in_at = {}
        interleave_at = {}
        quantise_x_at = {}
        for c in range(1, len(chunks)):
            for h in range(chunks[c][1] // PAIR):
                step = max(CHAN_TILES * c - FLIP_AHEAD + FLIP_STRIDE * h, 0)
                assert step not in flip_at
                flip_at[step] = chunks[c][0] // PAIR + h
            quantise_in_at[CHAN_TILES * c - PACK] = c
        windows = [(c, grp) for c in range(len(chunks)) for grp in range(PASSES)]
        for i in range(len(windows)):
            c, grp = windows[i]
            done = CHAN_TILES * c + PACK * (grp + 1)
            interleave_at[done] = (c, grp)
            if c == len(chunks) - 1:
                quantise_x_at[done + (PACK if grp == 0 else 1)] = (c, (grp,))
            elif grp == PASSES - 1:
                quantise_x_at[done + PACK] = (c, (0, 1))

        def keep_busy(n_matmuls):
            unread = second_psum.tile([P, WIDE], F32, tag="second")
            for m in range(n_matmuls):
                nc.tensor.matmul(out=unread[:], lhsT=blank[:, 0:P], rhs=blank[:], start=True, stop=True)

        keep_busy(WARM_BEFORE)
        for grp in range(PASSES):
            permute_scales(grp)
        permute_codes(0)
        for unit in range(chunks[0][1] // PAIR * PASSES):
            flip_inputs(unit, 1)
            quantise_unit(unit)
        keep_busy(WARM_BETWEEN)
        for part in range(1, len(PERMUTED)):
            permute_codes(part)
        nc.tensor.matmul(out=decay_psum[:], lhsT=ident_f32[:], rhs=decay[:], start=True, stop=True)
        issued = 0
        while issued < AHEAD:
            issued += first_layers(scans[issued][0], scans[issued][1])
        ready = 0
        multiplied = 0
        added = 0
        waiting = []
        for k in range(len(scans) + n_units):
            if k in quantise_x_at:
                c, passes = quantise_x_at[k]
                quantise_x(c, passes)
                grp = passes[-1]
                if c == len(chunks) - 1:
                    for n in range(n_units - TAIL_UNITS, n_units):
                        if grp == 0:
                            open_tail(n)
                        else:
                            second_pass(n, grp)
                    if grp == PASSES - 1:
                        assert multiplied == n_units - TAIL_UNITS
                        multiplied = n_units
                elif grp == PASSES - 1:
                    ready += chunks[c][1] // P * (FEAT // WIDE)
            if k in quantise_in_at:
                quantise_chunk(quantise_in_at[k])
            want = k + AHEAD + (1 if k in interleave_at else 0)
            while issued <= min(want, len(scans) - 1):
                issued += first_layers(scans[issued][0], scans[issued][1])
            if k < len(scans):
                recurrence(scans[k][0], scans[k][1])
            if k in interleave_at:
                c, grp = interleave_at[k]
                interleave_x(c, grp, 0)
                interleave_x(c, grp, 1)
            if waiting and (k % CHAN_TILES in ADD_STEPS or k >= max(interleave_at)):
                gpsimd_add(waiting[0])
                waiting = waiting[1:]
            if k in flip_at:
                flip_inputs(PASSES * flip_at[k], PASSES)
            lag = 1 if LAG_FROM <= k < len(scans) else 0
            if added < multiplied - lag:
                empty_bank(added)
                if not on_vector(added):
                    waiting.append(added)
                added += 1
            if multiplied < ready:
                second_matmul(multiplied)
                multiplied += 1
        assert not waiting
        assert added == n_units
